import numpy as np
import ml_dtypes


def mxq(x, axis, fmt="e4m3"):
    dtype, down = {"e4m3": (ml_dtypes.float8_e4m3fn, 7), "e5m2": (ml_dtypes.float8_e5m2, 14)}[fmt]
    v = np.moveaxis(np.asarray(x, np.float32).astype(ml_dtypes.bfloat16).astype(np.float64), axis, -1)
    blocks = v.reshape(v.shape[:-1] + (-1, 32))
    amax = np.abs(blocks).max(-1, keepdims=True)
    byte = np.maximum(np.where(amax > 0, np.frexp(amax)[1] - 1 + 127, 0) - down, 1)
    scale = np.exp2(byte - 127.0)
    codes = (blocks / scale).astype(np.float32).astype(dtype).astype(np.float64)
    return np.moveaxis((codes * scale).reshape(v.shape), -1, axis)


WIDE = False


def mx_kscale(k):
    if not WIDE:
        return np.ones(k)
    levels = np.array([10, -10, 5, -5, 0])
    a = np.random.permutation(np.resize(levels, k // 512 * 4)).reshape(k // 512, 4)
    idx = np.arange(k)
    return np.exp2(a[idx // 512, idx % 128 // 32])


BF16 = ml_dtypes.bfloat16


def bf(x):
    return np.asarray(x, np.float32).astype(BF16)


def f64(x):
    return np.asarray(x).astype(np.float64)


B, S, D, R = 8, 1024, 512, 8
EPS = 1e-6


def setup_inputs():
    s, t = mx_kscale(D), mx_kscale(D)
    return {"x": bf(np.random.standard_normal((B, S, D)) * s),
            "pos_emb": bf(np.random.standard_normal((1, S, D)) * s),
            "enc_w0": bf(np.random.standard_normal((D, D)) / np.sqrt(D) / s[None, :] * t[:, None]),
            "enc_w1": bf(np.random.standard_normal((D, D)) / np.sqrt(D) / t[None, :])}


def reference(x, pos_emb, enc_w0, enc_w1):
    x = f64(x)
    y = x + f64(pos_emb)[:, : x.shape[1]]
    h = np.maximum(mxq(y, 2, "e4m3") @ mxq(f64(enc_w0), 1, "e4m3").T, 0.0)
    h = np.maximum(mxq(h, 2, "e4m3") @ mxq(f64(enc_w1), 1, "e4m3").T, 0.0)
    return h / (np.sqrt((h * h).sum(-1, keepdims=True)) + EPS)

@@ -1,0 +1,191 @@
+from contextlib import ExitStack
+
+import concourse.mybir as mybir
+from concourse.masks import make_identity
+
+BF16 = mybir.dt.bfloat16
+F32 = mybir.dt.float32
+U32 = mybir.dt.uint32
+U8 = mybir.dt.uint8
+FP8X4 = mybir.dt.float8_e4m3fn_x4
+ACT = mybir.ActivationFunctionType
+ALU = mybir.AluOpType
+
+P = 128
+PACK = 4
+D = P * PACK
+HALVES = 2
+BATCH = 8
+SEQ = 1024
+TILES = SEQ // P
+PAIR = 2
+ROUND_TOKENS = PAIR * P
+ROUNDS_PER_BATCH = TILES // PAIR
+ROUNDS = BATCH * ROUNDS_PER_BATCH
+EPS = 1e-6
+TINY = 1e-30
+
+FLOPS = 2 * 2 * BATCH * SEQ * D * D
+
+
+def transpose_words(nc, dst, words, ident):
+    for u in range(HALVES):
+        nc.tensor.transpose(dst[:, u, :], words[:, u * P : (u + 1) * P], ident[:])
+
+
+def tile_mybadtransfomerblock_pa_t_kernel(tc, x, pos_emb, enc_w0, enc_w1, out):
+    nc = tc.nc
+    x_view = x.rearrange("b (p j) k -> b p j k", j=TILES)
+    pos_view = pos_emb.rearrange("o (p j) k -> o p j k", j=TILES)
+    out_view = out.rearrange("b (p j) f -> b p j f", j=TILES)
+
+    with ExitStack() as ctx:
+        keep = ctx.enter_context(tc.tile_pool(name="keep", bufs=1))
+        stage = ctx.enter_context(tc.tile_pool(name="stage", bufs=2))
+        rows = ctx.enter_context(tc.tile_pool(name="rows", bufs=4))
+        psum_t = ctx.enter_context(tc.psum_pool(name="psum_t", bufs=2))
+        psum_1 = ctx.enter_context(tc.psum_pool(name="psum_1", bufs=3))
+        psum_2 = ctx.enter_context(tc.psum_pool(name="psum_2", bufs=3))
+
+        w0_rows = keep.tile([P, PACK, D], BF16)
+        w0_view = enc_w0.rearrange("(u m e) k -> u m e k", u=HALVES, e=2)
+        for u in range(HALVES):
+            nc.sync.dma_start(out=w0_rows[:, 2 * u : 2 * u + 2, :], in_=w0_view[u])
+        w1_rows = keep.tile([P, PACK, D], BF16)
+        nc.sync.dma_start(out=w1_rows[:], in_=enc_w1.rearrange("(c m) k -> m c k", m=P))
+        pos_rows = keep.tile([P, TILES, D], BF16)
+        nc.sync.dma_start(out=pos_rows[:], in_=pos_view[0])
+        x_rows = []
+        for b in range(BATCH):
+            x_b = keep.tile([P, TILES, D], BF16, name="x%d" % b)
+            nc.sync.dma_start(out=x_b[:], in_=x_view[b])
+            x_rows.append(x_b)
+
+        ident = keep.tile([P, P], F32)
+        make_identity(nc, ident[:])
+        tiny = keep.tile([P, 1], F32)
+        nc.vector.memset(tiny[:], TINY)
+        warm = keep.tile([P, 1], F32)
+        nc.scalar.activation(out=warm[:], in_=tiny[:], func=ACT.Sqrt)
+
+        def spread(src_rows, n_tiles, grouped, copy):
+            src_words = src_rows[:].bitcast(F32)
+            grouped_words = grouped[:].bitcast(F32)
+            for h in range(n_tiles // PAIR):
+                t_bank = psum_t.tile([P, HALVES, ROUND_TOKENS], F32, tag="t_bank")
+                for i in range(PAIR):
+                    transpose_words(
+                        nc, t_bank[:, :, i * P : (i + 1) * P], src_words[:, PAIR * h + i, :], ident
+                    )
+                copy(
+                    out=grouped_words[:, h * ROUND_TOKENS : (h + 1) * ROUND_TOKENS, :],
+                    in_=t_bank[:].rearrange("p u r -> p r u"),
+                )
+
+        def quantise(grouped, width, name):
+            codes = keep.tile([P, width], U32, align_bytes=64, name=name + "_codes")
+            scales = keep.tile([P, width], U8, align_bytes=64, name=name + "_scales")
+            nc.vector.quantize_mx(
+                out=codes[:].bitcast(FP8X4),
+                scales=scales[:],
+                in_=grouped[:].rearrange("p c t -> p (c t)"),
+            )
+            return codes, scales
+
+        w0_grouped = keep.tile([P, D, PACK], BF16, align_bytes=64)
+        spread(w0_rows, PACK, w0_grouped, nc.vector.tensor_copy)
+        w1_grouped = keep.tile([P, D, PACK], BF16, align_bytes=64)
+        spread(w1_rows, PACK, w1_grouped, nc.vector.tensor_copy)
+        w0_codes, w0_scales = quantise(w0_grouped, D, "w0")
+        w1_codes, w1_scales = quantise(w1_grouped, D, "w1")
+        pos_grouped = keep.tile([P, SEQ, PACK], BF16)
+        spread(pos_rows, TILES, pos_grouped, nc.scalar.copy)
+
+        for r in range(ROUNDS):
+            b, q = divmod(r, ROUNDS_PER_BATCH)
+
+            x_words = x_rows[b][:].bitcast(F32)
+            t_bank = psum_t.tile([P, HALVES, ROUND_TOKENS], F32, tag="t_bank")
+            for i in range(PAIR):
+                transpose_words(
+                    nc, t_bank[:, :, i * P : (i + 1) * P], x_words[:, PAIR * q + i, :], ident
+                )
+
+            y_grouped = stage.tile([P, ROUND_TOKENS, PACK], BF16, align_bytes=64)
+            nc.vector.tensor_tensor(
+                out=y_grouped[:].rearrange("p r (u e) -> p r u e", u=HALVES),
+                in0=t_bank[:].bitcast(BF16).rearrange("p u (r e) -> p r u e", e=2),
+                in1=pos_grouped[:, q * ROUND_TOKENS : (q + 1) * ROUND_TOKENS, :].rearrange(
+                    "p r (u e) -> p r u e", u=HALVES
+                ),
+                op=ALU.add,
+            )
+            y_codes = stage.tile([P, ROUND_TOKENS], U32, align_bytes=64)
+            y_scales = stage.tile([P, ROUND_TOKENS], U8, align_bytes=64)
+            nc.vector.quantize_mx(
+                out=y_codes[:].bitcast(FP8X4),
+                scales=y_scales[:],
+                in_=y_grouped[:].rearrange("p r t -> p (r t)"),
+            )
+
+            h1_grouped = stage.tile([P, ROUND_TOKENS, PACK], BF16, align_bytes=64)
+            for i in range(PAIR):
+                tokens = slice(i * P, (i + 1) * P)
+                h1_bank = psum_1.tile([P, PACK, P], F32)
+                for t in range(PACK):
+                    nc.tensor.matmul_mx(
+                        out=h1_bank[:, t, :],
+                        lhsT=w0_codes[:, t * P : (t + 1) * P].bitcast(FP8X4),
+                        lhsT_scale=w0_scales[:, t * P : (t + 1) * P],
+                        rhs=y_codes[:, tokens].bitcast(FP8X4),
+                        rhs_scale=y_scales[:, tokens],
+                        start=True,
+                        stop=True,
+                    )
+                nc.vector.tensor_scalar_max(
+                    out=h1_grouped[:, tokens, :],
+                    in0=h1_bank[:].rearrange("p t r -> p r t"),
+                    scalar1=0.0,
+                )
+            h1_codes = stage.tile([P, ROUND_TOKENS], U32, align_bytes=64)
+            h1_scales = stage.tile([P, ROUND_TOKENS], U8, align_bytes=64)
+            nc.vector.quantize_mx(
+                out=h1_codes[:].bitcast(FP8X4),
+                scales=h1_scales[:],
+                in_=h1_grouped[:].rearrange("p r t -> p (r t)"),
+            )
+
+            h2_rows = rows.tile([P, PAIR, D], F32)
+            sumsq = rows.tile([P, PAIR], F32)
+            for i in range(PAIR):
+                tokens = slice(i * P, (i + 1) * P)
+                h2_bank = psum_2.tile([P, D], F32)
+                nc.tensor.matmul_mx(
+                    out=h2_bank[:],
+                    lhsT=h1_codes[:, tokens].bitcast(FP8X4),
+                    lhsT_scale=h1_scales[:, tokens],
+                    rhs=w1_codes[:].bitcast(FP8X4),
+                    rhs_scale=w1_scales[:],
+                    start=True,
+                    stop=True,
+                )
+                nc.scalar.activation(out=h2_rows[:, i, :], in_=h2_bank[:], func=ACT.Relu)
+            for i in range(PAIR):
+                squares = rows.tile([P, D], F32)
+                nc.scalar.activation(
+                    out=squares[:],
+                    in_=h2_rows[:, i, :],
+                    func=ACT.Square,
+                    accum_out=sumsq[:, i : i + 1],
+                )
+
+            norm = rows.tile([P, PAIR], F32)
+            nc.scalar.activation(out=norm[:], in_=sumsq[:], func=ACT.Sqrt, bias=tiny[:])
+            inv = rows.tile([P, PAIR], F32)
+            nc.vector.tensor_scalar_add(out=inv[:], in0=norm[:], scalar1=EPS)
+            nc.vector.reciprocal(out=inv[:], in_=inv[:])
+            for i in range(PAIR):
+                nc.vector.tensor_scalar_mul(
+                    out=h2_rows[:, i, :], in0=h2_rows[:, i, :], scalar1=inv[:, i : i + 1]
+                )
+            nc.sync.dma_start(out=out_view[b, :, PAIR * q : PAIR * (q + 1), :], in_=h2_rows[:])

@@ -28,11 +28,6 @@ TINY = 1e-30
 FLOPS = 2 * 2 * BATCH * SEQ * D * D
 
 
-def transpose_words(nc, dst, words, ident):
-    for u in range(HALVES):
-        nc.tensor.transpose(dst[:, u, :], words[:, u * P : (u + 1) * P], ident[:])
-
-
 def tile_mybadtransfomerblock_pa_t_kernel(tc, x, pos_emb, enc_w0, enc_w1, out):
     nc = tc.nc
     x_view = x.rearrange("b (p j) k -> b p j k", j=TILES)
@@ -54,12 +49,13 @@ def tile_mybadtransfomerblock_pa_t_kernel(tc, x, pos_emb, enc_w0, enc_w1, out):
         w1_rows = keep.tile([P, PACK, D], BF16)
         nc.sync.dma_start(out=w1_rows[:], in_=enc_w1.rearrange("(c m) k -> m c k", m=P))
         pos_rows = keep.tile([P, TILES, D], BF16)
-        nc.sync.dma_start(out=pos_rows[:], in_=pos_view[0])
-        x_rows = []
-        for b in range(BATCH):
-            x_b = keep.tile([P, TILES, D], BF16, name="x%d" % b)
-            nc.sync.dma_start(out=x_b[:], in_=x_view[b])
-            x_rows.append(x_b)
+        x_rows = [keep.tile([P, TILES, D], BF16, name="x%d" % b) for b in range(BATCH)]
+        for q in range(ROUNDS_PER_BATCH):
+            pair = slice(PAIR * q, PAIR * (q + 1))
+            nc.sync.dma_start(out=pos_rows[:, pair, :], in_=pos_view[0, :, pair, :])
+            nc.sync.dma_start(out=x_rows[0][:, pair, :], in_=x_view[0, :, pair, :])
+        for b in range(1, BATCH):
+            nc.sync.dma_start(out=x_rows[b][:], in_=x_view[b])
 
         ident = keep.tile([P, P], F32)
         make_identity(nc, ident[:])
@@ -68,23 +64,27 @@ def tile_mybadtransfomerblock_pa_t_kernel(tc, x, pos_emb, enc_w0, enc_w1, out):
         warm = keep.tile([P, 1], F32)
         nc.scalar.activation(out=warm[:], in_=tiny[:], func=ACT.Sqrt)
 
-        def spread(src_rows, n_tiles, grouped, copy):
+        def transpose_pair(src_rows, h):
             src_words = src_rows[:].bitcast(F32)
-            grouped_words = grouped[:].bitcast(F32)
-            for h in range(n_tiles // PAIR):
-                t_bank = psum_t.tile([P, HALVES, ROUND_TOKENS], F32, tag="t_bank")
-                for i in range(PAIR):
-                    transpose_words(
-                        nc, t_bank[:, :, i * P : (i + 1) * P], src_words[:, PAIR * h + i, :], ident
+            t_bank = psum_t.tile([P, HALVES, ROUND_TOKENS], F32)
+            for i in range(PAIR):
+                for u in range(HALVES):
+                    nc.tensor.transpose(
+                        t_bank[:, u, i * P : (i + 1) * P],
+                        src_words[:, PAIR * h + i, u * P : (u + 1) * P],
+                        ident[:],
                     )
-                copy(
-                    out=grouped_words[:, h * ROUND_TOKENS : (h + 1) * ROUND_TOKENS, :],
-                    in_=t_bank[:].rearrange("p u r -> p r u"),
-                )
+            return t_bank
 
-        def quantise(grouped, width, name):
-            codes = keep.tile([P, width], U32, align_bytes=64, name=name + "_codes")
-            scales = keep.tile([P, width], U8, align_bytes=64, name=name + "_scales")
+        def copy_grouped(copy, grouped, h, t_bank):
+            copy(
+                out=grouped[:].bitcast(F32)[:, h * ROUND_TOKENS : (h + 1) * ROUND_TOKENS, :],
+                in_=t_bank[:].rearrange("p u r -> p r u"),
+            )
+
+        def quantise(pool, grouped, width, name):
+            codes = pool.tile([P, width], U32, align_bytes=64, name=name + "_codes")
+            scales = pool.tile([P, width], U8, align_bytes=64, name=name + "_scales")
             nc.vector.quantize_mx(
                 out=codes[:].bitcast(FP8X4),
                 scales=scales[:],
@@ -93,42 +93,42 @@ def tile_mybadtransfomerblock_pa_t_kernel(tc, x, pos_emb, enc_w0, enc_w1, out):
             return codes, scales
 
         w0_grouped = keep.tile([P, D, PACK], BF16, align_bytes=64)
-        spread(w0_rows, PACK, w0_grouped, nc.vector.tensor_copy)
         w1_grouped = keep.tile([P, D, PACK], BF16, align_bytes=64)
-        spread(w1_rows, PACK, w1_grouped, nc.vector.tensor_copy)
-        w0_codes, w0_scales = quantise(w0_grouped, D, "w0")
-        w1_codes, w1_scales = quantise(w1_grouped, D, "w1")
+        for w_rows, w_grouped in ((w0_rows, w0_grouped), (w1_rows, w1_grouped)):
+            copy_grouped(nc.vector.tensor_copy, w_grouped, 0, transpose_pair(w_rows, 0))
+            copy_grouped(nc.scalar.copy, w_grouped, 1, transpose_pair(w_rows, 1))
+        w0_codes, w0_scales = quantise(keep, w0_grouped, D, "w0")
+        w1_codes, w1_scales = quantise(keep, w1_grouped, D, "w1")
         pos_grouped = keep.tile([P, SEQ, PACK], BF16)
-        spread(pos_rows, TILES, pos_grouped, nc.scalar.copy)
 
-        for r in range(ROUNDS):
+        xt_banks, y_tiles, y_mx, h1_banks, h1_tiles, h1_mx = {}, {}, {}, {}, {}, {}
+        h2_banks, h2_tiles, norms, invs = {}, {}, {}, {}
+
+        def transpose_x(r):
             b, q = divmod(r, ROUNDS_PER_BATCH)
+            if b == 0:
+                copy_grouped(nc.scalar.copy, pos_grouped, q, transpose_pair(pos_rows, q))
+            xt_banks[r] = transpose_pair(x_rows[b], q)
 
-            x_words = x_rows[b][:].bitcast(F32)
-            t_bank = psum_t.tile([P, HALVES, ROUND_TOKENS], F32, tag="t_bank")
-            for i in range(PAIR):
-                transpose_words(
-                    nc, t_bank[:, :, i * P : (i + 1) * P], x_words[:, PAIR * q + i, :], ident
-                )
-
+        def add_pos(r):
+            q = r % ROUNDS_PER_BATCH
             y_grouped = stage.tile([P, ROUND_TOKENS, PACK], BF16, align_bytes=64)
             nc.vector.tensor_tensor(
                 out=y_grouped[:].rearrange("p r (u e) -> p r u e", u=HALVES),
-                in0=t_bank[:].bitcast(BF16).rearrange("p u (r e) -> p r u e", e=2),
+                in0=xt_banks[r][:].bitcast(BF16).rearrange("p u (r e) -> p r u e", e=2),
                 in1=pos_grouped[:, q * ROUND_TOKENS : (q + 1) * ROUND_TOKENS, :].rearrange(
                     "p r (u e) -> p r u e", u=HALVES
                 ),
                 op=ALU.add,
             )
-            y_codes = stage.tile([P, ROUND_TOKENS], U32, align_bytes=64)
-            y_scales = stage.tile([P, ROUND_TOKENS], U8, align_bytes=64)
-            nc.vector.quantize_mx(
-                out=y_codes[:].bitcast(FP8X4),
-                scales=y_scales[:],
-                in_=y_grouped[:].rearrange("p r t -> p (r t)"),
-            )
+            y_tiles[r] = y_grouped
 
-            h1_grouped = stage.tile([P, ROUND_TOKENS, PACK], BF16, align_bytes=64)
+        def quantise_y(r):
+            y_mx[r] = quantise(stage, y_tiles[r], ROUND_TOKENS, "y")
+
+        def layer1(r):
+            y_codes, y_scales = y_mx[r]
+            h1_banks[r] = []
             for i in range(PAIR):
                 tokens = slice(i * P, (i + 1) * P)
                 h1_bank = psum_1.tile([P, PACK, P], F32)
@@ -142,21 +142,24 @@ def tile_mybadtransfomerblock_pa_t_kernel(tc, x, pos_emb, enc_w0, enc_w1, out):
                         start=True,
                         stop=True,
                     )
+                h1_banks[r].append(h1_bank)
+
+        def relu_h1(r):
+            h1_grouped = stage.tile([P, ROUND_TOKENS, PACK], BF16, align_bytes=64)
+            for i in range(PAIR):
                 nc.vector.tensor_scalar_max(
-                    out=h1_grouped[:, tokens, :],
-                    in0=h1_bank[:].rearrange("p t r -> p r t"),
+                    out=h1_grouped[:, i * P : (i + 1) * P, :],
+                    in0=h1_banks[r][i][:].rearrange("p t r -> p r t"),
                     scalar1=0.0,
                 )
-            h1_codes = stage.tile([P, ROUND_TOKENS], U32, align_bytes=64)
-            h1_scales = stage.tile([P, ROUND_TOKENS], U8, align_bytes=64)
-            nc.vector.quantize_mx(
-                out=h1_codes[:].bitcast(FP8X4),
-                scales=h1_scales[:],
-                in_=h1_grouped[:].rearrange("p r t -> p (r t)"),
-            )
+            h1_tiles[r] = h1_grouped
 
-            h2_rows = rows.tile([P, PAIR, D], F32)
-            sumsq = rows.tile([P, PAIR], F32)
+        def quantise_h1(r):
+            h1_mx[r] = quantise(stage, h1_tiles[r], ROUND_TOKENS, "h1")
+
+        def layer2(r):
+            h1_codes, h1_scales = h1_mx[r]
+            h2_banks[r] = []
             for i in range(PAIR):
                 tokens = slice(i * P, (i + 1) * P)
                 h2_bank = psum_2.tile([P, D], F32)
@@ -169,23 +172,61 @@ def tile_mybadtransfomerblock_pa_t_kernel(tc, x, pos_emb, enc_w0, enc_w1, out):
                     start=True,
                     stop=True,
                 )
-                nc.scalar.activation(out=h2_rows[:, i, :], in_=h2_bank[:], func=ACT.Relu)
+                h2_banks[r].append(h2_bank)
+
+        def relu_h2(r):
+            h2_rows = rows.tile([P, PAIR, D], F32)
+            for i in range(PAIR):
+                nc.scalar.activation(out=h2_rows[:, i, :], in_=h2_banks[r][i][:], func=ACT.Relu)
+            h2_tiles[r] = h2_rows
+
+        def norm_h2(r):
+            sumsq = rows.tile([P, PAIR], F32)
             for i in range(PAIR):
                 squares = rows.tile([P, D], F32)
                 nc.scalar.activation(
                     out=squares[:],
-                    in_=h2_rows[:, i, :],
+                    in_=h2_tiles[r][:, i, :],
                     func=ACT.Square,
                     accum_out=sumsq[:, i : i + 1],
                 )
-
             norm = rows.tile([P, PAIR], F32)
             nc.scalar.activation(out=norm[:], in_=sumsq[:], func=ACT.Sqrt, bias=tiny[:])
+            norms[r] = norm
+
+        def invert_norm(r):
             inv = rows.tile([P, PAIR], F32)
-            nc.vector.tensor_scalar_add(out=inv[:], in0=norm[:], scalar1=EPS)
+            nc.vector.tensor_scalar_add(out=inv[:], in0=norms[r][:], scalar1=EPS)
             nc.vector.reciprocal(out=inv[:], in_=inv[:])
+            invs[r] = inv
+
+        def scale_and_store(r):
+            b, q = divmod(r, ROUNDS_PER_BATCH)
+            h2_rows = h2_tiles[r]
             for i in range(PAIR):
-                nc.vector.tensor_scalar_mul(
-                    out=h2_rows[:, i, :], in0=h2_rows[:, i, :], scalar1=inv[:, i : i + 1]
+                nc.gpsimd.tensor_scalar(
+                    out=h2_rows[:, i, :],
+                    in0=h2_rows[:, i, :],
+                    scalar1=invs[r][:, i : i + 1],
+                    scalar2=0.0,
+                    op0=ALU.mult,
+                    op1=ALU.add,
                 )
             nc.sync.dma_start(out=out_view[b, :, PAIR * q : PAIR * (q + 1), :], in_=h2_rows[:])
+
+        def run(stage_fn, r):
+            if 0 <= r < ROUNDS:
+                stage_fn(r)
+
+        for r in range(ROUNDS):
+            transpose_x(r)
+            add_pos(r)
+            quantise_y(r)
+            layer1(r)
+            relu_h1(r)
+            quantise_h1(r)
+            layer2(r)
+            relu_h2(r)
+            norm_h2(r)
+            invert_norm(r)
+            scale_and_store(r)

@@ -41,6 +41,7 @@ def tile_mybadtransfomerblock_pa_t_kernel(tc, x, pos_emb, enc_w0, enc_w1, out):
         psum_t = ctx.enter_context(tc.psum_pool(name="psum_t", bufs=2))
         psum_1 = ctx.enter_context(tc.psum_pool(name="psum_1", bufs=3))
         psum_2 = ctx.enter_context(tc.psum_pool(name="psum_2", bufs=3))
+        ctx.enter_context(tc.manual_schedule())
 
         w0_rows = keep.tile([P, PACK, D], BF16)
         w0_view = enc_w0.rearrange("(u m e) k -> u m e k", u=HALVES, e=2)
@@ -218,15 +219,15 @@ def tile_mybadtransfomerblock_pa_t_kernel(tc, x, pos_emb, enc_w0, enc_w1, out):
             if 0 <= r < ROUNDS:
                 stage_fn(r)
 
-        for r in range(ROUNDS):
-            transpose_x(r)
-            add_pos(r)
-            quantise_y(r)
-            layer1(r)
-            relu_h1(r)
-            quantise_h1(r)
-            layer2(r)
-            relu_h2(r)
-            norm_h2(r)
-            invert_norm(r)
-            scale_and_store(r)
+        for s in range(ROUNDS + 4):
+            run(layer1, s - 2)
+            run(layer2, s - 3)
+            run(transpose_x, s)
+            run(add_pos, s - 1)
+            run(relu_h1, s - 2)
+            run(quantise_y, s - 1)
+            run(quantise_h1, s - 2)
+            run(relu_h2, s - 3)
+            run(norm_h2, s - 3)
+            run(invert_norm, s - 4)
+            run(scale_and_store, s - 4)

@@ -37,7 +37,7 @@ def tile_mybadtransfomerblock_pa_t_kernel(tc, x, pos_emb, enc_w0, enc_w1, out):
     with ExitStack() as ctx:
         keep = ctx.enter_context(tc.tile_pool(name="keep", bufs=1))
         stage = ctx.enter_context(tc.tile_pool(name="stage", bufs=2))
-        rows = ctx.enter_context(tc.tile_pool(name="rows", bufs=4))
+        rows = ctx.enter_context(tc.tile_pool(name="rows", bufs=6))
         psum_t = ctx.enter_context(tc.psum_pool(name="psum_t", bufs=2))
         psum_1 = ctx.enter_context(tc.psum_pool(name="psum_1", bufs=3))
         psum_2 = ctx.enter_context(tc.psum_pool(name="psum_2", bufs=3))
@@ -103,7 +103,7 @@ def tile_mybadtransfomerblock_pa_t_kernel(tc, x, pos_emb, enc_w0, enc_w1, out):
         pos_grouped = keep.tile([P, SEQ, PACK], BF16)
 
         xt_banks, y_tiles, y_mx, h1_banks, h1_tiles, h1_mx = {}, {}, {}, {}, {}, {}
-        h2_banks, h2_tiles, norms, invs = {}, {}, {}, {}
+        h2_banks, h2_tiles, sumsqs, norms, paddeds, invs = {}, {}, {}, {}, {}, {}
 
         def transpose_x(r):
             b, q = divmod(r, ROUNDS_PER_BATCH)
@@ -191,14 +191,21 @@ def tile_mybadtransfomerblock_pa_t_kernel(tc, x, pos_emb, enc_w0, enc_w1, out):
                     func=ACT.Square,
                     accum_out=sumsq[:, i : i + 1],
                 )
+            sumsqs[r] = sumsq
+
+        def root_norm(r):
             norm = rows.tile([P, PAIR], F32)
-            nc.scalar.activation(out=norm[:], in_=sumsq[:], func=ACT.Sqrt, bias=tiny[:])
+            nc.scalar.activation(out=norm[:], in_=sumsqs[r][:], func=ACT.Sqrt, bias=tiny[:])
             norms[r] = norm
+
+        def pad_norm(r):
+            padded = rows.tile([P, PAIR], F32)
+            nc.vector.tensor_scalar_add(out=padded[:], in0=norms[r][:], scalar1=EPS)
+            paddeds[r] = padded
 
         def invert_norm(r):
             inv = rows.tile([P, PAIR], F32)
-            nc.vector.tensor_scalar_add(out=inv[:], in0=norms[r][:], scalar1=EPS)
-            nc.vector.reciprocal(out=inv[:], in_=inv[:])
+            nc.vector.reciprocal(out=inv[:], in_=paddeds[r][:])
             invs[r] = inv
 
         def scale_and_store(r):
@@ -219,15 +226,17 @@ def tile_mybadtransfomerblock_pa_t_kernel(tc, x, pos_emb, enc_w0, enc_w1, out):
             if 0 <= r < ROUNDS:
                 stage_fn(r)
 
-        for s in range(ROUNDS + 4):
+        for s in range(ROUNDS + 7):
             run(layer1, s - 2)
             run(layer2, s - 3)
             run(transpose_x, s)
+            run(invert_norm, s - 6)
             run(add_pos, s - 1)
             run(relu_h1, s - 2)
             run(quantise_y, s - 1)
+            run(pad_norm, s - 5)
             run(quantise_h1, s - 2)
+            run(root_norm, s - 4)
             run(relu_h2, s - 3)
             run(norm_h2, s - 3)
-            run(invert_norm, s - 4)
-            run(scale_and_store, s - 4)
+            run(scale_and_store, s - 6)

@@ -23,6 +23,8 @@ ROUND_TOKENS = PAIR * P
 ROUNDS_PER_BATCH = TILES // PAIR
 ROUNDS = BATCH * ROUNDS_PER_BATCH
 EPS = 1e-6
+FILL_ROUNDS = 3
+DRAIN_ROUNDS = 3
 TINY = 1e-30
 
 FLOPS = 2 * 2 * BATCH * SEQ * D * D
@@ -145,15 +147,23 @@ def tile_mybadtransfomerblock_pa_t_kernel(tc, x, pos_emb, enc_w0, enc_w1, out):
                     )
                 h1_banks[r].append(h1_bank)
 
-        def relu_h1(r):
+        def relu_h1_scalar(r):
             h1_grouped = stage.tile([P, ROUND_TOKENS, PACK], BF16, align_bytes=64)
-            for i in range(PAIR):
+            h1_tiles[r] = h1_grouped
+            if r < FILL_ROUNDS:
+                nc.scalar.activation(
+                    out=h1_grouped[:, P : 2 * P, :],
+                    in_=h1_banks[r][1][:].rearrange("p t r -> p r t"),
+                    func=ACT.Relu,
+                )
+
+        def relu_h1_vector(r):
+            for i in range(1 if r < FILL_ROUNDS else PAIR):
                 nc.vector.tensor_scalar_max(
-                    out=h1_grouped[:, i * P : (i + 1) * P, :],
+                    out=h1_tiles[r][:, i * P : (i + 1) * P, :],
                     in0=h1_banks[r][i][:].rearrange("p t r -> p r t"),
                     scalar1=0.0,
                 )
-            h1_tiles[r] = h1_grouped
 
         def quantise_h1(r):
             h1_mx[r] = quantise(stage, h1_tiles[r], ROUND_TOKENS, "h1")
@@ -175,15 +185,24 @@ def tile_mybadtransfomerblock_pa_t_kernel(tc, x, pos_emb, enc_w0, enc_w1, out):
                 )
                 h2_banks[r].append(h2_bank)
 
-        def relu_h2(r):
+        def relu_h2_first(r):
             h2_rows = rows.tile([P, PAIR, D], F32)
-            for i in range(PAIR):
-                nc.scalar.activation(out=h2_rows[:, i, :], in_=h2_banks[r][i][:], func=ACT.Relu)
+            nc.scalar.activation(out=h2_rows[:, 0, :], in_=h2_banks[r][0][:], func=ACT.Relu)
             h2_tiles[r] = h2_rows
 
-        def norm_h2(r):
+        def relu_h2_second(r):
+            if r < ROUNDS - 1:
+                nc.scalar.activation(out=h2_tiles[r][:, 1, :], in_=h2_banks[r][1][:], func=ACT.Relu)
+
+        def relu_h2_vector(r):
+            if r == ROUNDS - 1:
+                nc.vector.tensor_scalar_max(
+                    out=h2_tiles[r][:, 1, :], in0=h2_banks[r][1][:], scalar1=0.0
+                )
+
+        def squares_scalar(r):
             sumsq = rows.tile([P, PAIR], F32)
-            for i in range(PAIR):
+            for i in range(1 if r >= ROUNDS - DRAIN_ROUNDS else PAIR):
                 squares = rows.tile([P, D], F32)
                 nc.scalar.activation(
                     out=squares[:],
@@ -192,6 +211,19 @@ def tile_mybadtransfomerblock_pa_t_kernel(tc, x, pos_emb, enc_w0, enc_w1, out):
                     accum_out=sumsq[:, i : i + 1],
                 )
             sumsqs[r] = sumsq
+
+        def squares_vector(r):
+            if r >= ROUNDS - DRAIN_ROUNDS:
+                products = rows.tile([P, D], F32)
+                nc.vector.scalar_tensor_tensor(
+                    out=products[:],
+                    in0=h2_tiles[r][:, 1, :],
+                    scalar=1.0,
+                    in1=h2_tiles[r][:, 1, :],
+                    op0=ALU.mult,
+                    op1=ALU.mult,
+                    accum_out=sumsqs[r][:, 1:2],
+                )
 
         def root_norm(r):
             norm = rows.tile([P, PAIR], F32)
@@ -208,10 +240,19 @@ def tile_mybadtransfomerblock_pa_t_kernel(tc, x, pos_emb, enc_w0, enc_w1, out):
             nc.vector.reciprocal(out=inv[:], in_=paddeds[r][:])
             invs[r] = inv
 
+        def scale_vector(r):
+            if r >= ROUNDS - DRAIN_ROUNDS:
+                b, q = divmod(r, ROUNDS_PER_BATCH)
+                nc.vector.tensor_scalar_mul(
+                    out=h2_tiles[r][:, 1, :], in0=h2_tiles[r][:, 1, :], scalar1=invs[r][:, 1:2]
+                )
+                nc.sync.dma_start(out=out_view[b, :, PAIR * q + 1, :], in_=h2_tiles[r][:, 1, :])
+
         def scale_and_store(r):
             b, q = divmod(r, ROUNDS_PER_BATCH)
             h2_rows = h2_tiles[r]
-            for i in range(PAIR):
+            shared = r >= ROUNDS - DRAIN_ROUNDS
+            for i in range(1 if shared else PAIR):
                 nc.gpsimd.tensor_scalar(
                     out=h2_rows[:, i, :],
                     in0=h2_rows[:, i, :],
@@ -220,23 +261,31 @@ def tile_mybadtransfomerblock_pa_t_kernel(tc, x, pos_emb, enc_w0, enc_w1, out):
                     op0=ALU.mult,
                     op1=ALU.add,
                 )
-            nc.sync.dma_start(out=out_view[b, :, PAIR * q : PAIR * (q + 1), :], in_=h2_rows[:])
+            if shared:
+                nc.sync.dma_start(out=out_view[b, :, PAIR * q, :], in_=h2_rows[:, 0, :])
+            else:
+                nc.sync.dma_start(out=out_view[b, :, PAIR * q : PAIR * (q + 1), :], in_=h2_rows[:])
 
         def run(stage_fn, r):
             if 0 <= r < ROUNDS:
                 stage_fn(r)
 
-        for s in range(ROUNDS + 7):
+        for s in range(ROUNDS + 6):
             run(layer1, s - 2)
             run(layer2, s - 3)
             run(transpose_x, s)
-            run(invert_norm, s - 6)
-            run(add_pos, s - 1)
-            run(relu_h1, s - 2)
-            run(quantise_y, s - 1)
+            run(relu_h1_scalar, s - 2)
+            run(squares_vector, s - 4)
             run(pad_norm, s - 5)
+            run(add_pos, s - 1)
+            run(invert_norm, s - 5)
+            run(scale_vector, s - 5)
+            run(relu_h1_vector, s - 2)
+            run(quantise_y, s - 1)
             run(quantise_h1, s - 2)
+            run(relu_h2_first, s - 3)
+            run(relu_h2_vector, s - 3)
             run(root_norm, s - 4)
-            run(relu_h2, s - 3)
-            run(norm_h2, s - 3)
-            run(scale_and_store, s - 6)
+            run(relu_h2_second, s - 3)
+            run(squares_scalar, s - 3)
+            run(scale_and_store, s - 5)

@@ -67,9 +67,19 @@ def tile_mybadtransfomerblock_pa_t_kernel(tc, x, pos_emb, enc_w0, enc_w1, out):
         warm = keep.tile([P, 1], F32)
         nc.scalar.activation(out=warm[:], in_=tiny[:], func=ACT.Sqrt)
 
-        def transpose_pair(src_rows, h):
+        def transpose_pair(src_rows, h, keep_busy=False):
             src_words = src_rows[:].bitcast(F32)
             t_bank = psum_t.tile([P, HALVES, ROUND_TOKENS], F32)
+            if keep_busy:
+                nc.tensor.matmul_mx(
+                    out=t_bank[:].rearrange("p u r -> p (u r)"),
+                    lhsT=w0_codes[:, :P].bitcast(FP8X4),
+                    lhsT_scale=w0_scales[:, :P],
+                    rhs=w1_codes[:].bitcast(FP8X4),
+                    rhs_scale=w1_scales[:],
+                    start=True,
+                    stop=True,
+                )
             for i in range(PAIR):
                 for u in range(HALVES):
                     nc.tensor.transpose(
@@ -111,7 +121,7 @@ def tile_mybadtransfomerblock_pa_t_kernel(tc, x, pos_emb, enc_w0, enc_w1, out):
             b, q = divmod(r, ROUNDS_PER_BATCH)
             if b == 0:
                 copy_grouped(nc.scalar.copy, pos_grouped, q, transpose_pair(pos_rows, q))
-            xt_banks[r] = transpose_pair(x_rows[b], q)
+            xt_banks[r] = transpose_pair(x_rows[b], q, keep_busy=r >= FILL_ROUNDS)
 
         def add_pos(r):
             q = r % ROUNDS_PER_BATCH

@@ -69,10 +69,10 @@ def tile_mybadtransfomerblock_pa_t_kernel(tc, x, pos_emb, enc_w0, enc_w1, out):
 
         def transpose_pair(src_rows, h, keep_busy=False):
             src_words = src_rows[:].bitcast(F32)
-            t_bank = psum_t.tile([P, HALVES, ROUND_TOKENS], F32)
+            t_bank = psum_t.tile([P, ROUND_TOKENS, HALVES], F32)
             if keep_busy:
                 nc.tensor.matmul_mx(
-                    out=t_bank[:].rearrange("p u r -> p (u r)"),
+                    out=t_bank[:].rearrange("p r u -> p (r u)"),
                     lhsT=w0_codes[:, :P].bitcast(FP8X4),
                     lhsT_scale=w0_scales[:, :P],
                     rhs=w1_codes[:].bitcast(FP8X4),
@@ -83,7 +83,7 @@ def tile_mybadtransfomerblock_pa_t_kernel(tc, x, pos_emb, enc_w0, enc_w1, out):
             for i in range(PAIR):
                 for u in range(HALVES):
                     nc.tensor.transpose(
-                        t_bank[:, u, i * P : (i + 1) * P],
+                        t_bank[:, i * P : (i + 1) * P, u],
                         src_words[:, PAIR * h + i, u * P : (u + 1) * P],
                         ident[:],
                     )
@@ -92,7 +92,7 @@ def tile_mybadtransfomerblock_pa_t_kernel(tc, x, pos_emb, enc_w0, enc_w1, out):
         def copy_grouped(copy, grouped, h, t_bank):
             copy(
                 out=grouped[:].bitcast(F32)[:, h * ROUND_TOKENS : (h + 1) * ROUND_TOKENS, :],
-                in_=t_bank[:].rearrange("p u r -> p r u"),
+                in_=t_bank[:],
             )
 
         def quantise(pool, grouped, width, name):
@@ -127,11 +127,9 @@ def tile_mybadtransfomerblock_pa_t_kernel(tc, x, pos_emb, enc_w0, enc_w1, out):
             q = r % ROUNDS_PER_BATCH
             y_grouped = stage.tile([P, ROUND_TOKENS, PACK], BF16, align_bytes=64)
             nc.vector.tensor_tensor(
-                out=y_grouped[:].rearrange("p r (u e) -> p r u e", u=HALVES),
-                in0=xt_banks[r][:].bitcast(BF16).rearrange("p u (r e) -> p r u e", e=2),
-                in1=pos_grouped[:, q * ROUND_TOKENS : (q + 1) * ROUND_TOKENS, :].rearrange(
-                    "p r (u e) -> p r u e", u=HALVES
-                ),
+                out=y_grouped[:],
+                in0=xt_banks[r][:].bitcast(BF16),
+                in1=pos_grouped[:, q * ROUND_TOKENS : (q + 1) * ROUND_TOKENS, :],
                 op=ALU.add,
             )
             y_tiles[r] = y_grouped

@@ -23,7 +23,7 @@ ROUND_TOKENS = PAIR * P
 ROUNDS_PER_BATCH = TILES // PAIR
 ROUNDS = BATCH * ROUNDS_PER_BATCH
 EPS = 1e-6
-FILL_ROUNDS = 3
+FILL_ROUNDS = 2
 DRAIN_ROUNDS = 3
 TINY = 1e-30
 
@@ -35,6 +35,10 @@ def tile_mybadtransfomerblock_pa_t_kernel(tc, x, pos_emb, enc_w0, enc_w1, out):
     x_view = x.rearrange("b (p j) k -> b p j k", j=TILES)
     pos_view = pos_emb.rearrange("o (p j) k -> o p j k", j=TILES)
     out_view = out.rearrange("b (p j) f -> b p j f", j=TILES)
+
+    def place(r):
+        q, b = divmod(r, BATCH)
+        return b, q
 
     with ExitStack() as ctx:
         keep = ctx.enter_context(tc.tile_pool(name="keep", bufs=1))
@@ -50,15 +54,31 @@ def tile_mybadtransfomerblock_pa_t_kernel(tc, x, pos_emb, enc_w0, enc_w1, out):
         for u in range(HALVES):
             nc.sync.dma_start(out=w0_rows[:, 2 * u : 2 * u + 2, :], in_=w0_view[u])
         w1_rows = keep.tile([P, PACK, D], BF16)
-        nc.sync.dma_start(out=w1_rows[:], in_=enc_w1.rearrange("(c m) k -> m c k", m=P))
         pos_rows = keep.tile([P, TILES, D], BF16)
         x_rows = [keep.tile([P, TILES, D], BF16, name="x%d" % b) for b in range(BATCH)]
-        for q in range(ROUNDS_PER_BATCH):
+
+        def load_x(b, first, last):
+            nc.sync.dma_start(
+                out=x_rows[b][:, PAIR * first : PAIR * last, :],
+                in_=x_view[b, :, PAIR * first : PAIR * last, :],
+            )
+
+        def load_pos(q):
             pair = slice(PAIR * q, PAIR * (q + 1))
             nc.sync.dma_start(out=pos_rows[:, pair, :], in_=pos_view[0, :, pair, :])
-            nc.sync.dma_start(out=x_rows[0][:, pair, :], in_=x_view[0, :, pair, :])
-        for b in range(1, BATCH):
-            nc.sync.dma_start(out=x_rows[b][:], in_=x_view[b])
+
+        load_pos(0)
+        load_x(0, 0, 1)
+        load_x(1, 0, 1)
+        for q in range(1, ROUNDS_PER_BATCH):
+            load_pos(q)
+        nc.sync.dma_start(out=w1_rows[:], in_=enc_w1.rearrange("(c m) k -> m c k", m=P))
+        for b in range(2, BATCH):
+            load_x(b, 0, 1)
+        for b in range(BATCH):
+            load_x(b, 1, 2)
+        for b in range(BATCH):
+            load_x(b, 2, ROUNDS_PER_BATCH)
 
         ident = keep.tile([P, P], F32)
         make_identity(nc, ident[:])
@@ -67,19 +87,8 @@ def tile_mybadtransfomerblock_pa_t_kernel(tc, x, pos_emb, enc_w0, enc_w1, out):
         warm = keep.tile([P, 1], F32)
         nc.scalar.activation(out=warm[:], in_=tiny[:], func=ACT.Sqrt)
 
-        def transpose_pair(src_rows, h, keep_busy=False):
+        def transpose_pair(src_rows, h, t_bank):
             src_words = src_rows[:].bitcast(F32)
-            t_bank = psum_t.tile([P, ROUND_TOKENS, HALVES], F32)
-            if keep_busy:
-                nc.tensor.matmul_mx(
-                    out=t_bank[:].rearrange("p r u -> p (r u)"),
-                    lhsT=w0_codes[:, :P].bitcast(FP8X4),
-                    lhsT_scale=w0_scales[:, :P],
-                    rhs=w1_codes[:].bitcast(FP8X4),
-                    rhs_scale=w1_scales[:],
-                    start=True,
-                    stop=True,
-                )
             for i in range(PAIR):
                 for u in range(HALVES):
                     nc.tensor.transpose(
@@ -105,26 +114,19 @@ def tile_mybadtransfomerblock_pa_t_kernel(tc, x, pos_emb, enc_w0, enc_w1, out):
             )
             return codes, scales
 
-        w0_grouped = keep.tile([P, D, PACK], BF16, align_bytes=64)
-        w1_grouped = keep.tile([P, D, PACK], BF16, align_bytes=64)
-        for w_rows, w_grouped in ((w0_rows, w0_grouped), (w1_rows, w1_grouped)):
-            copy_grouped(nc.vector.tensor_copy, w_grouped, 0, transpose_pair(w_rows, 0))
-            copy_grouped(nc.scalar.copy, w_grouped, 1, transpose_pair(w_rows, 1))
-        w0_codes, w0_scales = quantise(keep, w0_grouped, D, "w0")
-        w1_codes, w1_scales = quantise(keep, w1_grouped, D, "w1")
-        pos_grouped = keep.tile([P, SEQ, PACK], BF16)
-
         xt_banks, y_tiles, y_mx, h1_banks, h1_tiles, h1_mx = {}, {}, {}, {}, {}, {}
         h2_banks, h2_tiles, sumsqs, norms, paddeds, invs = {}, {}, {}, {}, {}, {}
 
         def transpose_x(r):
-            b, q = divmod(r, ROUNDS_PER_BATCH)
-            if b == 0:
-                copy_grouped(nc.scalar.copy, pos_grouped, q, transpose_pair(pos_rows, q))
-            xt_banks[r] = transpose_pair(x_rows[b], q, keep_busy=r >= FILL_ROUNDS)
+            b, q = place(r)
+            t_bank = psum_t.tile([P, ROUND_TOKENS, HALVES], F32)
+            xt_banks[r] = transpose_pair(x_rows[b], q, t_bank)
+
+        def prepare_pos(q, t_bank):
+            copy_grouped(nc.scalar.copy, pos_grouped, q, transpose_pair(pos_rows, q, t_bank))
 
         def add_pos(r):
-            q = r % ROUNDS_PER_BATCH
+            q = place(r)[1]
             y_grouped = stage.tile([P, ROUND_TOKENS, PACK], BF16, align_bytes=64)
             nc.vector.tensor_tensor(
                 out=y_grouped[:],
@@ -158,7 +160,7 @@ def tile_mybadtransfomerblock_pa_t_kernel(tc, x, pos_emb, enc_w0, enc_w1, out):
         def relu_h1_scalar(r):
             h1_grouped = stage.tile([P, ROUND_TOKENS, PACK], BF16, align_bytes=64)
             h1_tiles[r] = h1_grouped
-            if r < FILL_ROUNDS:
+            if 0 < r < FILL_ROUNDS:
                 nc.scalar.activation(
                     out=h1_grouped[:, P : 2 * P, :],
                     in_=h1_banks[r][1][:].rearrange("p t r -> p r t"),
@@ -166,7 +168,7 @@ def tile_mybadtransfomerblock_pa_t_kernel(tc, x, pos_emb, enc_w0, enc_w1, out):
                 )
 
         def relu_h1_vector(r):
-            for i in range(1 if r < FILL_ROUNDS else PAIR):
+            for i in range(1 if 0 < r < FILL_ROUNDS else PAIR):
                 nc.vector.tensor_scalar_max(
                     out=h1_tiles[r][:, i * P : (i + 1) * P, :],
                     in0=h1_banks[r][i][:].rearrange("p t r -> p r t"),
@@ -250,14 +252,14 @@ def tile_mybadtransfomerblock_pa_t_kernel(tc, x, pos_emb, enc_w0, enc_w1, out):
 
         def scale_vector(r):
             if r >= ROUNDS - DRAIN_ROUNDS:
-                b, q = divmod(r, ROUNDS_PER_BATCH)
+                b, q = place(r)
                 nc.vector.tensor_scalar_mul(
                     out=h2_tiles[r][:, 1, :], in0=h2_tiles[r][:, 1, :], scalar1=invs[r][:, 1:2]
                 )
                 nc.sync.dma_start(out=out_view[b, :, PAIR * q + 1, :], in_=h2_tiles[r][:, 1, :])
 
         def scale_and_store(r):
-            b, q = divmod(r, ROUNDS_PER_BATCH)
+            b, q = place(r)
             h2_rows = h2_tiles[r]
             shared = r >= ROUNDS - DRAIN_ROUNDS
             for i in range(1 if shared else PAIR):
@@ -278,22 +280,68 @@ def tile_mybadtransfomerblock_pa_t_kernel(tc, x, pos_emb, enc_w0, enc_w1, out):
             if 0 <= r < ROUNDS:
                 stage_fn(r)
 
-        for s in range(ROUNDS + 6):
-            run(layer1, s - 2)
-            run(layer2, s - 3)
+        w0_grouped = keep.tile([P, D, PACK], BF16, align_bytes=64)
+        w1_grouped = keep.tile([P, D, PACK], BF16, align_bytes=64)
+        w0_codes = keep.tile([P, D], U32, align_bytes=64)
+        w0_scales = keep.tile([P, D], U8, align_bytes=64)
+        pos_grouped = keep.tile([P, SEQ, PACK], BF16)
+        w0_banks = []
+        for h in range(2):
+            h2_bank = psum_2.tile([P, ROUND_TOKENS, HALVES], F32)
+            w0_banks.append(transpose_pair(w0_rows, h, h2_bank))
+        h1_bank = psum_1.tile([P, ROUND_TOKENS, HALVES], F32)
+        copy_grouped(nc.vector.tensor_copy, w0_grouped, 0, w0_banks[0])
+        copy_grouped(nc.scalar.copy, w0_grouped, 1, w0_banks[1])
+        prepare_pos(0, h1_bank)
+        transpose_x(0)
+        transpose_x(1)
+        h2_bank = psum_2.tile([P, ROUND_TOKENS, HALVES], F32)
+        prepare_pos(1, h2_bank)
+        h1_bank = psum_1.tile([P, ROUND_TOKENS, HALVES], F32)
+        prepare_pos(2, h1_bank)
+        for h in range(2):
+            half = slice(h * ROUND_TOKENS, (h + 1) * ROUND_TOKENS)
+            nc.vector.quantize_mx(
+                out=w0_codes[:, half].bitcast(FP8X4),
+                scales=w0_scales[:, half],
+                in_=w0_grouped[:, half, :].rearrange("p c t -> p (c t)"),
+            )
+        add_pos(0)
+        add_pos(1)
+        quantise_y(0)
+        quantise_y(1)
+        layer1(0)
+        h2_bank = psum_2.tile([P, ROUND_TOKENS, HALVES], F32)
+        prepare_pos(3, h2_bank)
+        relu_h1_scalar(0)
+        relu_h1_vector(0)
+        for h in range(2):
+            h2_bank = psum_2.tile([P, ROUND_TOKENS, HALVES], F32)
+            copy_grouped(nc.scalar.copy, w1_grouped, h, transpose_pair(w1_rows, h, h2_bank))
+        transpose_x(2)
+        layer1(1)
+        add_pos(2)
+        quantise_h1(0)
+        w1_codes, w1_scales = quantise(keep, w1_grouped, D, "w1")
+
+        for s in range(3, ROUNDS + 7):
             run(transpose_x, s)
+            if s > 3:
+                run(layer1, s - 2)
+            run(layer2, s - 3)
             run(relu_h1_scalar, s - 2)
             run(squares_vector, s - 4)
-            run(pad_norm, s - 5)
-            run(add_pos, s - 1)
-            run(invert_norm, s - 5)
-            run(scale_vector, s - 5)
+            run(invert_norm, s - 6)
+            if s > 3:
+                run(add_pos, s - 1)
+            run(scale_vector, s - 6)
             run(relu_h1_vector, s - 2)
             run(quantise_y, s - 1)
+            run(pad_norm, s - 5)
             run(quantise_h1, s - 2)
             run(relu_h2_first, s - 3)
             run(relu_h2_vector, s - 3)
             run(root_norm, s - 4)
             run(relu_h2_second, s - 3)
             run(squares_scalar, s - 3)
-            run(scale_and_store, s - 5)
+            run(scale_and_store, s - 6)

@@ -20,11 +20,10 @@ SEQ = 1024
 TILES = SEQ // P
 PAIR = 2
 ROUND_TOKENS = PAIR * P
-ROUNDS_PER_BATCH = TILES // PAIR
-ROUNDS = BATCH * ROUNDS_PER_BATCH
+PAIRS = TILES // PAIR
+ROUNDS = BATCH * PAIRS
+LAST = ROUNDS - 1
 EPS = 1e-6
-FILL_ROUNDS = 2
-DRAIN_ROUNDS = 3
 TINY = 1e-30
 
 FLOPS = 2 * 2 * BATCH * SEQ * D * D
@@ -50,9 +49,6 @@ def tile_mybadtransfomerblock_pa_t_kernel(tc, x, pos_emb, enc_w0, enc_w1, out):
         ctx.enter_context(tc.manual_schedule())
 
         w0_rows = keep.tile([P, PACK, D], BF16)
-        w0_view = enc_w0.rearrange("(u m e) k -> u m e k", u=HALVES, e=2)
-        for u in range(HALVES):
-            nc.sync.dma_start(out=w0_rows[:, 2 * u : 2 * u + 2, :], in_=w0_view[u])
         w1_rows = keep.tile([P, PACK, D], BF16)
         pos_rows = keep.tile([P, TILES, D], BF16)
         x_rows = [keep.tile([P, TILES, D], BF16, name="x%d" % b) for b in range(BATCH)]
@@ -67,10 +63,13 @@ def tile_mybadtransfomerblock_pa_t_kernel(tc, x, pos_emb, enc_w0, enc_w1, out):
             pair = slice(PAIR * q, PAIR * (q + 1))
             nc.sync.dma_start(out=pos_rows[:, pair, :], in_=pos_view[0, :, pair, :])
 
+        w0_view = enc_w0.rearrange("(u m e) k -> u m e k", u=HALVES, e=2)
+        for u in range(HALVES):
+            nc.sync.dma_start(out=w0_rows[:, 2 * u : 2 * u + 2, :], in_=w0_view[u])
         load_pos(0)
         load_x(0, 0, 1)
         load_x(1, 0, 1)
-        for q in range(1, ROUNDS_PER_BATCH):
+        for q in range(1, PAIRS):
             load_pos(q)
         nc.sync.dma_start(out=w1_rows[:], in_=enc_w1.rearrange("(c m) k -> m c k", m=P))
         for b in range(2, BATCH):
@@ -78,7 +77,7 @@ def tile_mybadtransfomerblock_pa_t_kernel(tc, x, pos_emb, enc_w0, enc_w1, out):
         for b in range(BATCH):
             load_x(b, 1, 2)
         for b in range(BATCH):
-            load_x(b, 2, ROUNDS_PER_BATCH)
+            load_x(b, 2, PAIRS)
 
         ident = keep.tile([P, P], F32)
         make_identity(nc, ident[:])
@@ -104,15 +103,12 @@ def tile_mybadtransfomerblock_pa_t_kernel(tc, x, pos_emb, enc_w0, enc_w1, out):
                 in_=t_bank[:],
             )
 
-        def quantise(pool, grouped, width, name):
-            codes = pool.tile([P, width], U32, align_bytes=64, name=name + "_codes")
-            scales = pool.tile([P, width], U8, align_bytes=64, name=name + "_scales")
+        def quantise(codes, scales, grouped):
             nc.vector.quantize_mx(
-                out=codes[:].bitcast(FP8X4),
-                scales=scales[:],
-                in_=grouped[:].rearrange("p c t -> p (c t)"),
+                out=codes.bitcast(FP8X4),
+                scales=scales,
+                in_=grouped.rearrange("p c t -> p (c t)"),
             )
-            return codes, scales
 
         xt_banks, y_tiles, y_mx, h1_banks, h1_tiles, h1_mx = {}, {}, {}, {}, {}, {}
         h2_banks, h2_tiles, sumsqs, norms, paddeds, invs = {}, {}, {}, {}, {}, {}
@@ -137,7 +133,10 @@ def tile_mybadtransfomerblock_pa_t_kernel(tc, x, pos_emb, enc_w0, enc_w1, out):
             y_tiles[r] = y_grouped
 
         def quantise_y(r):
-            y_mx[r] = quantise(stage, y_tiles[r], ROUND_TOKENS, "y")
+            y_codes = stage.tile([P, ROUND_TOKENS], U32, align_bytes=64)
+            y_scales = stage.tile([P, ROUND_TOKENS], U8, align_bytes=64)
+            quantise(y_codes[:], y_scales[:], y_tiles[r][:])
+            y_mx[r] = y_codes, y_scales
 
         def layer1(r):
             y_codes, y_scales = y_mx[r]
@@ -157,33 +156,40 @@ def tile_mybadtransfomerblock_pa_t_kernel(tc, x, pos_emb, enc_w0, enc_w1, out):
                     )
                 h1_banks[r].append(h1_bank)
 
-        def relu_h1_scalar(r):
+        def open_h1(r):
             h1_grouped = stage.tile([P, ROUND_TOKENS, PACK], BF16, align_bytes=64)
             h1_tiles[r] = h1_grouped
-            if 0 < r < FILL_ROUNDS:
-                nc.scalar.activation(
-                    out=h1_grouped[:, P : 2 * P, :],
-                    in_=h1_banks[r][1][:].rearrange("p t r -> p r t"),
-                    func=ACT.Relu,
-                )
 
-        def relu_h1_vector(r):
-            for i in range(1 if 0 < r < FILL_ROUNDS else PAIR):
-                nc.vector.tensor_scalar_max(
-                    out=h1_tiles[r][:, i * P : (i + 1) * P, :],
-                    in0=h1_banks[r][i][:].rearrange("p t r -> p r t"),
-                    scalar1=0.0,
-                )
+        def relu_h1_scalar(r, i):
+            nc.scalar.activation(
+                out=h1_tiles[r][:, i * P : (i + 1) * P, :],
+                in_=h1_banks[r][i][:].rearrange("p t r -> p r t"),
+                func=ACT.Relu,
+            )
+
+        def relu_h1_vector(r, i):
+            nc.vector.tensor_scalar_max(
+                out=h1_tiles[r][:, i * P : (i + 1) * P, :],
+                in0=h1_banks[r][i][:].rearrange("p t r -> p r t"),
+                scalar1=0.0,
+            )
 
         def quantise_h1(r):
-            h1_mx[r] = quantise(stage, h1_tiles[r], ROUND_TOKENS, "h1")
+            h1_codes = stage.tile([P, ROUND_TOKENS], U32, align_bytes=64)
+            h1_scales = stage.tile([P, ROUND_TOKENS], U8, align_bytes=64)
+            quantise(h1_codes[:], h1_scales[:], h1_tiles[r][:])
+            h1_mx[r] = h1_codes, h1_scales
 
         def layer2(r):
             h1_codes, h1_scales = h1_mx[r]
             h2_banks[r] = []
             for i in range(PAIR):
                 tokens = slice(i * P, (i + 1) * P)
-                h2_bank = psum_2.tile([P, D], F32)
+                if r < LAST:
+                    h2_bank = psum_2.tile([P, D], F32)
+                else:
+                    t_bank = psum_t.tile([P, D], F32)
+                    h2_bank = t_bank
                 nc.tensor.matmul_mx(
                     out=h2_bank[:],
                     lhsT=h1_codes[:, tokens].bitcast(FP8X4),
@@ -195,45 +201,39 @@ def tile_mybadtransfomerblock_pa_t_kernel(tc, x, pos_emb, enc_w0, enc_w1, out):
                 )
                 h2_banks[r].append(h2_bank)
 
-        def relu_h2_first(r):
+        def open_h2(r):
             h2_rows = rows.tile([P, PAIR, D], F32)
-            nc.scalar.activation(out=h2_rows[:, 0, :], in_=h2_banks[r][0][:], func=ACT.Relu)
-            h2_tiles[r] = h2_rows
-
-        def relu_h2_second(r):
-            if r < ROUNDS - 1:
-                nc.scalar.activation(out=h2_tiles[r][:, 1, :], in_=h2_banks[r][1][:], func=ACT.Relu)
-
-        def relu_h2_vector(r):
-            if r == ROUNDS - 1:
-                nc.vector.tensor_scalar_max(
-                    out=h2_tiles[r][:, 1, :], in0=h2_banks[r][1][:], scalar1=0.0
-                )
-
-        def squares_scalar(r):
             sumsq = rows.tile([P, PAIR], F32)
-            for i in range(1 if r >= ROUNDS - DRAIN_ROUNDS else PAIR):
-                squares = rows.tile([P, D], F32)
-                nc.scalar.activation(
-                    out=squares[:],
-                    in_=h2_tiles[r][:, i, :],
-                    func=ACT.Square,
-                    accum_out=sumsq[:, i : i + 1],
-                )
-            sumsqs[r] = sumsq
+            h2_tiles[r], sumsqs[r] = h2_rows, sumsq
 
-        def squares_vector(r):
-            if r >= ROUNDS - DRAIN_ROUNDS:
-                products = rows.tile([P, D], F32)
-                nc.vector.scalar_tensor_tensor(
-                    out=products[:],
-                    in0=h2_tiles[r][:, 1, :],
-                    scalar=1.0,
-                    in1=h2_tiles[r][:, 1, :],
-                    op0=ALU.mult,
-                    op1=ALU.mult,
-                    accum_out=sumsqs[r][:, 1:2],
-                )
+        def relu_h2_scalar(r, i):
+            nc.scalar.activation(out=h2_tiles[r][:, i, :], in_=h2_banks[r][i][:], func=ACT.Relu)
+
+        def relu_h2_vector(r, i):
+            nc.vector.tensor_scalar_max(
+                out=h2_tiles[r][:, i, :], in0=h2_banks[r][i][:], scalar1=0.0
+            )
+
+        def square_scalar(r, i):
+            squares = rows.tile([P, D], F32)
+            nc.scalar.activation(
+                out=squares[:],
+                in_=h2_tiles[r][:, i, :],
+                func=ACT.Square,
+                accum_out=sumsqs[r][:, i : i + 1],
+            )
+
+        def square_vector(r, i):
+            products = rows.tile([P, D], F32)
+            nc.vector.scalar_tensor_tensor(
+                out=products[:],
+                in0=h2_tiles[r][:, i, :],
+                scalar=1.0,
+                in1=h2_tiles[r][:, i, :],
+                op0=ALU.mult,
+                op1=ALU.mult,
+                accum_out=sumsqs[r][:, i : i + 1],
+            )
 
         def root_norm(r):
             norm = rows.tile([P, PAIR], F32)
@@ -250,98 +250,177 @@ def tile_mybadtransfomerblock_pa_t_kernel(tc, x, pos_emb, enc_w0, enc_w1, out):
             nc.vector.reciprocal(out=inv[:], in_=paddeds[r][:])
             invs[r] = inv
 
-        def scale_vector(r):
-            if r >= ROUNDS - DRAIN_ROUNDS:
-                b, q = place(r)
-                nc.vector.tensor_scalar_mul(
-                    out=h2_tiles[r][:, 1, :], in0=h2_tiles[r][:, 1, :], scalar1=invs[r][:, 1:2]
-                )
-                nc.sync.dma_start(out=out_view[b, :, PAIR * q + 1, :], in_=h2_tiles[r][:, 1, :])
+        def scale_vector(r, i):
+            nc.vector.tensor_scalar_mul(
+                out=h2_tiles[r][:, i, :], in0=h2_tiles[r][:, i, :], scalar1=invs[r][:, i : i + 1]
+            )
+
+        def scale_gpsimd(r, i):
+            nc.gpsimd.tensor_scalar(
+                out=h2_tiles[r][:, i, :],
+                in0=h2_tiles[r][:, i, :],
+                scalar1=invs[r][:, i : i + 1],
+                scalar2=0.0,
+                op0=ALU.mult,
+                op1=ALU.add,
+            )
+
+        def scale_scalar(r, i):
+            nc.scalar.activation(
+                out=h2_tiles[r][:, i, :],
+                in_=h2_tiles[r][:, i, :],
+                func=ACT.Copy,
+                scale=invs[r][:, i : i + 1],
+            )
+
+        def store(r):
+            b, q = place(r)
+            nc.sync.dma_start(
+                out=out_view[b, :, PAIR * q : PAIR * (q + 1), :], in_=h2_tiles[r][:]
+            )
+
+        def store_tile(r, i):
+            b, q = place(r)
+            nc.sync.dma_start(out=out_view[b, :, PAIR * q + i, :], in_=h2_tiles[r][:, i, :])
 
         def scale_and_store(r):
-            b, q = place(r)
-            h2_rows = h2_tiles[r]
-            shared = r >= ROUNDS - DRAIN_ROUNDS
-            for i in range(1 if shared else PAIR):
-                nc.gpsimd.tensor_scalar(
-                    out=h2_rows[:, i, :],
-                    in0=h2_rows[:, i, :],
-                    scalar1=invs[r][:, i : i + 1],
-                    scalar2=0.0,
-                    op0=ALU.mult,
-                    op1=ALU.add,
-                )
-            if shared:
-                nc.sync.dma_start(out=out_view[b, :, PAIR * q, :], in_=h2_rows[:, 0, :])
-            else:
-                nc.sync.dma_start(out=out_view[b, :, PAIR * q : PAIR * (q + 1), :], in_=h2_rows[:])
+            for i in range(PAIR):
+                scale_gpsimd(r, i)
+            store(r)
 
-        def run(stage_fn, r):
+        def run(stage_fn, r, *rest):
             if 0 <= r < ROUNDS:
-                stage_fn(r)
+                stage_fn(r, *rest)
 
         w0_grouped = keep.tile([P, D, PACK], BF16, align_bytes=64)
         w1_grouped = keep.tile([P, D, PACK], BF16, align_bytes=64)
         w0_codes = keep.tile([P, D], U32, align_bytes=64)
         w0_scales = keep.tile([P, D], U8, align_bytes=64)
+        w1_codes = keep.tile([P, D], U32, align_bytes=64)
+        w1_scales = keep.tile([P, D], U8, align_bytes=64)
         pos_grouped = keep.tile([P, SEQ, PACK], BF16)
-        w0_banks = []
-        for h in range(2):
+
+        def spare_bank_1():
+            h1_bank = psum_1.tile([P, ROUND_TOKENS, HALVES], F32)
+            return h1_bank
+
+        def spare_bank_2():
             h2_bank = psum_2.tile([P, ROUND_TOKENS, HALVES], F32)
-            w0_banks.append(transpose_pair(w0_rows, h, h2_bank))
-        h1_bank = psum_1.tile([P, ROUND_TOKENS, HALVES], F32)
-        copy_grouped(nc.vector.tensor_copy, w0_grouped, 0, w0_banks[0])
-        copy_grouped(nc.scalar.copy, w0_grouped, 1, w0_banks[1])
-        prepare_pos(0, h1_bank)
+            return h2_bank
+
+        copy_grouped(nc.vector.tensor_copy, w0_grouped, 0, transpose_pair(w0_rows, 0, spare_bank_2()))
+        copy_grouped(nc.scalar.copy, w0_grouped, 1, transpose_pair(w0_rows, 1, spare_bank_2()))
+        prepare_pos(0, spare_bank_1())
         transpose_x(0)
         transpose_x(1)
-        h2_bank = psum_2.tile([P, ROUND_TOKENS, HALVES], F32)
-        prepare_pos(1, h2_bank)
-        h1_bank = psum_1.tile([P, ROUND_TOKENS, HALVES], F32)
-        prepare_pos(2, h1_bank)
+        prepare_pos(1, spare_bank_2())
+        prepare_pos(2, spare_bank_1())
         for h in range(2):
             half = slice(h * ROUND_TOKENS, (h + 1) * ROUND_TOKENS)
-            nc.vector.quantize_mx(
-                out=w0_codes[:, half].bitcast(FP8X4),
-                scales=w0_scales[:, half],
-                in_=w0_grouped[:, half, :].rearrange("p c t -> p (c t)"),
-            )
+            quantise(w0_codes[:, half], w0_scales[:, half], w0_grouped[:, half, :])
         add_pos(0)
         add_pos(1)
         quantise_y(0)
         quantise_y(1)
         layer1(0)
-        h2_bank = psum_2.tile([P, ROUND_TOKENS, HALVES], F32)
-        prepare_pos(3, h2_bank)
-        relu_h1_scalar(0)
-        relu_h1_vector(0)
+        prepare_pos(3, spare_bank_2())
+        open_h1(0)
+        for i in range(PAIR):
+            relu_h1_vector(0, i)
         for h in range(2):
-            h2_bank = psum_2.tile([P, ROUND_TOKENS, HALVES], F32)
-            copy_grouped(nc.scalar.copy, w1_grouped, h, transpose_pair(w1_rows, h, h2_bank))
+            copy_grouped(nc.scalar.copy, w1_grouped, h, transpose_pair(w1_rows, h, spare_bank_2()))
         transpose_x(2)
         layer1(1)
         add_pos(2)
         quantise_h1(0)
-        w1_codes, w1_scales = quantise(keep, w1_grouped, D, "w1")
+        quantise(w1_codes[:], w1_scales[:], w1_grouped[:])
+        transpose_x(3)
+        layer2(0)
+        open_h1(1)
+        relu_h1_scalar(1, 1)
+        relu_h1_vector(1, 0)
+        quantise_y(2)
+        quantise_h1(1)
+        open_h2(0)
+        for i in range(PAIR):
+            relu_h2_scalar(0, i)
+        for i in range(PAIR):
+            square_scalar(0, i)
 
-        for s in range(3, ROUNDS + 7):
-            run(transpose_x, s)
-            if s > 3:
-                run(layer1, s - 2)
-            run(layer2, s - 3)
-            run(relu_h1_scalar, s - 2)
-            run(squares_vector, s - 4)
+        for s in range(4, ROUNDS):
+            transpose_x(s)
+            layer1(s - 2)
+            layer2(s - 3)
             run(invert_norm, s - 6)
-            if s > 3:
-                run(add_pos, s - 1)
-            run(scale_vector, s - 6)
-            run(relu_h1_vector, s - 2)
-            run(quantise_y, s - 1)
+            add_pos(s - 1)
+            open_h1(s - 2)
+            for i in range(PAIR):
+                relu_h1_vector(s - 2, i)
+            quantise_y(s - 1)
             run(pad_norm, s - 5)
-            run(quantise_h1, s - 2)
-            run(relu_h2_first, s - 3)
-            run(relu_h2_vector, s - 3)
-            run(root_norm, s - 4)
-            run(relu_h2_second, s - 3)
-            run(squares_scalar, s - 3)
+            quantise_h1(s - 2)
+            open_h2(s - 3)
+            relu_h2_scalar(s - 3, 0)
+            root_norm(s - 4)
+            relu_h2_scalar(s - 3, 1)
+            for i in range(PAIR):
+                square_scalar(s - 3, i)
             run(scale_and_store, s - 6)
+
+        layer1(LAST - 1)
+        layer2(LAST - 2)
+        invert_norm(LAST - 5)
+        scale_and_store(LAST - 5)
+        add_pos(LAST)
+        open_h1(LAST - 1)
+        for i in range(PAIR):
+            relu_h1_vector(LAST - 1, i)
+        quantise_y(LAST)
+        pad_norm(LAST - 4)
+        quantise_h1(LAST - 1)
+        open_h2(LAST - 2)
+        relu_h2_scalar(LAST - 2, 0)
+        root_norm(LAST - 3)
+        relu_h2_scalar(LAST - 2, 1)
+        for i in range(PAIR):
+            square_scalar(LAST - 2, i)
+        layer1(LAST)
+        layer2(LAST - 1)
+        invert_norm(LAST - 4)
+        scale_and_store(LAST - 4)
+        open_h1(LAST)
+        for i in range(PAIR):
+            relu_h1_vector(LAST, i)
+        pad_norm(LAST - 3)
+        quantise_h1(LAST)
+        invert_norm(LAST - 3)
+        scale_and_store(LAST - 3)
+        open_h2(LAST - 1)
+        relu_h2_scalar(LAST - 1, 0)
+        relu_h2_vector(LAST - 1, 1)
+        layer2(LAST)
+        open_h2(LAST)
+        root_norm(LAST - 2)
+        square_scalar(LAST - 1, 0)
+        relu_h2_vector(LAST, 0)
+        pad_norm(LAST - 2)
+        relu_h2_vector(LAST, 1)
+        invert_norm(LAST - 2)
+        square_scalar(LAST - 1, 1)
+        square_scalar(LAST, 0)
+        root_norm(LAST - 1)
+        square_scalar(LAST, 1)
+        root_norm(LAST)
+        for i in range(PAIR):
+            scale_vector(LAST - 2, i)
+        store(LAST - 2)
+        pad_norm(LAST - 1)
+        invert_norm(LAST - 1)
+        scale_vector(LAST - 1, 0)
+        pad_norm(LAST)
+        scale_vector(LAST - 1, 1)
+        store(LAST - 1)
+        invert_norm(LAST)
+        for i, scale in enumerate((scale_vector, scale_scalar)):
+            scale(LAST, i)
+            store_tile(LAST, i)

@@ -23,6 +23,7 @@ ROUND_TOKENS = PAIR * P
 PAIRS = TILES // PAIR
 ROUNDS = BATCH * PAIRS
 LAST = ROUNDS - 1
+AWAKE_FIRST = 6
 EPS = 1e-6
 TINY = 1e-30
 
@@ -79,6 +80,8 @@ def tile_mybadtransfomerblock_pa_t_kernel(tc, x, pos_emb, enc_w0, enc_w1, out):
         for b in range(BATCH):
             load_x(b, 2, PAIRS)
 
+        zeros = keep.tile([P, D], BF16)
+        nc.vector.memset(zeros[:], 0.0)
         ident = keep.tile([P, P], F32)
         make_identity(nc, ident[:])
         tiny = keep.tile([P, 1], F32)
@@ -308,11 +311,20 @@ def tile_mybadtransfomerblock_pa_t_kernel(tc, x, pos_emb, enc_w0, enc_w1, out):
             h2_bank = psum_2.tile([P, ROUND_TOKENS, HALVES], F32)
             return h2_bank
 
+        def keep_awake(passes):
+            for i in range(passes):
+                nc.tensor.matmul(
+                    idle_bank[:], lhsT=zeros[:, :P], rhs=zeros[:], start=True, stop=True
+                )
+
+        idle_bank = psum_1.tile([P, D], F32, name="h1_bank")
+        keep_awake(AWAKE_FIRST)
         copy_grouped(nc.vector.tensor_copy, w0_grouped, 0, transpose_pair(w0_rows, 0, spare_bank_2()))
         copy_grouped(nc.scalar.copy, w0_grouped, 1, transpose_pair(w0_rows, 1, spare_bank_2()))
         prepare_pos(0, spare_bank_1())
         transpose_x(0)
         transpose_x(1)
+        keep_awake(2)
         prepare_pos(1, spare_bank_2())
         prepare_pos(2, spare_bank_1())
         for h in range(2):

@@ -70,10 +70,11 @@ def tile_mybadtransfomerblock_pa_t_kernel(tc, x, pos_emb, enc_w0, enc_w1, out):
         load_pos(0)
         load_x(0, 0, 1)
         load_x(1, 0, 1)
-        for q in range(1, PAIRS):
-            load_pos(q)
         nc.sync.dma_start(out=w1_rows[:], in_=enc_w1.rearrange("(c m) k -> m c k", m=P))
-        for b in range(2, BATCH):
+        for q in range(1, PAIRS):
+            load_x(q + 1, 0, 1)
+            load_pos(q)
+        for b in range(PAIRS + 1, BATCH):
             load_x(b, 0, 1)
         for b in range(BATCH):
             load_x(b, 1, 2)
@@ -248,6 +249,11 @@ def tile_mybadtransfomerblock_pa_t_kernel(tc, x, pos_emb, enc_w0, enc_w1, out):
             nc.vector.tensor_scalar_add(out=padded[:], in0=norms[r][:], scalar1=EPS)
             paddeds[r] = padded
 
+        def pad_norm_scalar(r):
+            padded = rows.tile([P, PAIR], F32)
+            nc.scalar.activation(out=padded[:], in_=norms[r][:], func=ACT.Copy, bias=EPS)
+            paddeds[r] = padded
+
         def invert_norm(r):
             inv = rows.tile([P, PAIR], F32)
             nc.vector.reciprocal(out=inv[:], in_=paddeds[r][:])
@@ -325,8 +331,8 @@ def tile_mybadtransfomerblock_pa_t_kernel(tc, x, pos_emb, enc_w0, enc_w1, out):
         transpose_x(0)
         transpose_x(1)
         keep_awake(2)
-        prepare_pos(1, spare_bank_2())
-        prepare_pos(2, spare_bank_1())
+        for h in range(2):
+            copy_grouped(nc.scalar.copy, w1_grouped, h, transpose_pair(w1_rows, h, spare_bank_2()))
         for h in range(2):
             half = slice(h * ROUND_TOKENS, (h + 1) * ROUND_TOKENS)
             quantise(w0_codes[:, half], w0_scales[:, half], w0_grouped[:, half, :])
@@ -335,51 +341,55 @@ def tile_mybadtransfomerblock_pa_t_kernel(tc, x, pos_emb, enc_w0, enc_w1, out):
         quantise_y(0)
         quantise_y(1)
         layer1(0)
-        prepare_pos(3, spare_bank_2())
         open_h1(0)
-        for i in range(PAIR):
-            relu_h1_vector(0, i)
-        for h in range(2):
-            copy_grouped(nc.scalar.copy, w1_grouped, h, transpose_pair(w1_rows, h, spare_bank_2()))
+        relu_h1_vector(0, 0)
+        relu_h1_scalar(0, 1)
         transpose_x(2)
+        prepare_pos(1, spare_bank_2())
         layer1(1)
-        add_pos(2)
-        quantise_h1(0)
         quantise(w1_codes[:], w1_scales[:], w1_grouped[:])
-        transpose_x(3)
+        quantise_h1(0)
         layer2(0)
+        transpose_x(3)
+        add_pos(2)
         open_h1(1)
-        relu_h1_scalar(1, 1)
         relu_h1_vector(1, 0)
+        relu_h1_scalar(1, 1)
         quantise_y(2)
+        layer1(2)
         quantise_h1(1)
-        open_h2(0)
-        for i in range(PAIR):
-            relu_h2_scalar(0, i)
-        for i in range(PAIR):
-            square_scalar(0, i)
+
+        def scalar_stages(r):
+            open_h2(r)
+            relu_h2_scalar(r, 0)
+            run(root_norm, r - 1)
+            relu_h2_scalar(r, 1)
+            if r % 2 == 0:
+                run(pad_norm_scalar, r - 1)
+            for i in range(PAIR):
+                square_scalar(r, i)
 
         for s in range(4, ROUNDS):
             transpose_x(s)
-            layer1(s - 2)
+            if s > 4:
+                layer1(s - 2)
+            open_h1(s - 2)
+            scalar_stages(s - 4)
+            if s - 2 < PAIRS:
+                prepare_pos(s - 2, spare_bank_2())
             layer2(s - 3)
             run(invert_norm, s - 6)
             add_pos(s - 1)
-            open_h1(s - 2)
             for i in range(PAIR):
                 relu_h1_vector(s - 2, i)
             quantise_y(s - 1)
-            run(pad_norm, s - 5)
+            if s % 2 == 1:
+                run(pad_norm, s - 5)
             quantise_h1(s - 2)
-            open_h2(s - 3)
-            relu_h2_scalar(s - 3, 0)
-            root_norm(s - 4)
-            relu_h2_scalar(s - 3, 1)
-            for i in range(PAIR):
-                square_scalar(s - 3, i)
             run(scale_and_store, s - 6)
 
         layer1(LAST - 1)
+        scalar_stages(LAST - 3)
         layer2(LAST - 2)
         invert_norm(LAST - 5)
         scale_and_store(LAST - 5)
@@ -388,15 +398,9 @@ def tile_mybadtransfomerblock_pa_t_kernel(tc, x, pos_emb, enc_w0, enc_w1, out):
         for i in range(PAIR):
             relu_h1_vector(LAST - 1, i)
         quantise_y(LAST)
-        pad_norm(LAST - 4)
         quantise_h1(LAST - 1)
-        open_h2(LAST - 2)
-        relu_h2_scalar(LAST - 2, 0)
-        root_norm(LAST - 3)
-        relu_h2_scalar(LAST - 2, 1)
-        for i in range(PAIR):
-            square_scalar(LAST - 2, i)
         layer1(LAST)
+        scalar_stages(LAST - 2)
         layer2(LAST - 1)
         invert_norm(LAST - 4)
         scale_and_store(LAST - 4)
@@ -425,14 +429,16 @@ def tile_mybadtransfomerblock_pa_t_kernel(tc, x, pos_emb, enc_w0, enc_w1, out):
         root_norm(LAST)
         for i in range(PAIR):
             scale_vector(LAST - 2, i)
-        store(LAST - 2)
+            store_tile(LAST - 2, i)
         pad_norm(LAST - 1)
         invert_norm(LAST - 1)
         scale_vector(LAST - 1, 0)
+        store_tile(LAST - 1, 0)
         pad_norm(LAST)
         scale_vector(LAST - 1, 1)
-        store(LAST - 1)
+        store_tile(LAST - 1, 1)
         invert_norm(LAST)
-        for i, scale in enumerate((scale_vector, scale_scalar)):
-            scale(LAST, i)
-            store_tile(LAST, i)
+        scale_vector(LAST, 0)
+        store_tile(LAST, 0)
+        scale_scalar(LAST, 1)
+        store_tile(LAST, 1)

@@ -371,36 +371,37 @@ def tile_mybadtransfomerblock_pa_t_kernel(tc, x, pos_emb, enc_w0, enc_w1, out):
 
         for s in range(4, ROUNDS):
             transpose_x(s)
-            if s > 4:
-                layer1(s - 2)
-            open_h1(s - 2)
             scalar_stages(s - 4)
             if s - 2 < PAIRS:
                 prepare_pos(s - 2, spare_bank_2())
-            layer2(s - 3)
-            run(invert_norm, s - 6)
             add_pos(s - 1)
+            if s % 2 == 0:
+                run(pad_norm, s - 6)
+            if s > 4:
+                quantise_h1(s - 3)
+            layer2(s - 3)
+            quantise_y(s - 1)
+            run(invert_norm, s - 6)
+            open_h1(s - 2)
             for i in range(PAIR):
                 relu_h1_vector(s - 2, i)
-            quantise_y(s - 1)
-            if s % 2 == 1:
-                run(pad_norm, s - 5)
-            quantise_h1(s - 2)
+            layer1(s - 1)
             run(scale_and_store, s - 6)
 
-        layer1(LAST - 1)
         scalar_stages(LAST - 3)
+        add_pos(LAST)
+        pad_norm(LAST - 5)
+        quantise_h1(LAST - 2)
         layer2(LAST - 2)
+        quantise_y(LAST)
         invert_norm(LAST - 5)
         scale_and_store(LAST - 5)
-        add_pos(LAST)
         open_h1(LAST - 1)
         for i in range(PAIR):
             relu_h1_vector(LAST - 1, i)
-        quantise_y(LAST)
-        quantise_h1(LAST - 1)
         layer1(LAST)
         scalar_stages(LAST - 2)
+        quantise_h1(LAST - 1)
         layer2(LAST - 1)
         invert_norm(LAST - 4)
         scale_and_store(LAST - 4)
@@ -429,16 +430,14 @@ def tile_mybadtransfomerblock_pa_t_kernel(tc, x, pos_emb, enc_w0, enc_w1, out):
         root_norm(LAST)
         for i in range(PAIR):
             scale_vector(LAST - 2, i)
-            store_tile(LAST - 2, i)
+        store(LAST - 2)
         pad_norm(LAST - 1)
         invert_norm(LAST - 1)
         scale_vector(LAST - 1, 0)
-        store_tile(LAST - 1, 0)
         pad_norm(LAST)
         scale_vector(LAST - 1, 1)
-        store_tile(LAST - 1, 1)
+        store(LAST - 1)
         invert_norm(LAST)
-        scale_vector(LAST, 0)
-        store_tile(LAST, 0)
-        scale_scalar(LAST, 1)
-        store_tile(LAST, 1)
+        for i, scale in enumerate((scale_vector, scale_scalar)):
+            scale(LAST, i)
+            store_tile(LAST, i)

@@ -400,7 +400,12 @@ def tile_mybadtransfomerblock_pa_t_kernel(tc, x, pos_emb, enc_w0, enc_w1, out):
         for i in range(PAIR):
             relu_h1_vector(LAST - 1, i)
         layer1(LAST)
-        scalar_stages(LAST - 2)
+        open_h2(LAST - 2)
+        relu_h2_scalar(LAST - 2, 0)
+        root_norm(LAST - 3)
+        relu_h2_scalar(LAST - 2, 1)
+        for i in range(PAIR):
+            square_scalar(LAST - 2, i)
         quantise_h1(LAST - 1)
         layer2(LAST - 1)
         invert_norm(LAST - 4)
@@ -413,12 +418,12 @@ def tile_mybadtransfomerblock_pa_t_kernel(tc, x, pos_emb, enc_w0, enc_w1, out):
         invert_norm(LAST - 3)
         scale_and_store(LAST - 3)
         open_h2(LAST - 1)
-        relu_h2_scalar(LAST - 1, 0)
+        relu_h2_vector(LAST - 1, 0)
         relu_h2_vector(LAST - 1, 1)
         layer2(LAST)
         open_h2(LAST)
-        root_norm(LAST - 2)
         square_scalar(LAST - 1, 0)
+        root_norm(LAST - 2)
         relu_h2_vector(LAST, 0)
         pad_norm(LAST - 2)
         relu_h2_vector(LAST, 1)

@@ -43,7 +43,7 @@ def tile_mybadtransfomerblock_pa_t_kernel(tc, x, pos_emb, enc_w0, enc_w1, out):
     with ExitStack() as ctx:
         keep = ctx.enter_context(tc.tile_pool(name="keep", bufs=1))
         stage = ctx.enter_context(tc.tile_pool(name="stage", bufs=2))
-        rows = ctx.enter_context(tc.tile_pool(name="rows", bufs=6))
+        rows = ctx.enter_context(tc.tile_pool(name="rows", bufs=12))
         psum_t = ctx.enter_context(tc.psum_pool(name="psum_t", bufs=2))
         psum_1 = ctx.enter_context(tc.psum_pool(name="psum_1", bufs=3))
         psum_2 = ctx.enter_context(tc.psum_pool(name="psum_2", bufs=3))
@@ -76,10 +76,13 @@ def tile_mybadtransfomerblock_pa_t_kernel(tc, x, pos_emb, enc_w0, enc_w1, out):
             load_pos(q)
         for b in range(PAIRS + 1, BATCH):
             load_x(b, 0, 1)
-        for b in range(BATCH):
-            load_x(b, 1, 2)
-        for b in range(BATCH):
-            load_x(b, 2, PAIRS)
+
+        def load_ahead(r):
+            b, q = place(r)
+            if q == 1:
+                load_x(b, 1, 2)
+            elif q == 2:
+                load_x(b, 2, PAIRS)
 
         zeros = keep.tile([P, D], BF16)
         nc.vector.memset(zeros[:], 0.0)
@@ -219,7 +222,7 @@ def tile_mybadtransfomerblock_pa_t_kernel(tc, x, pos_emb, enc_w0, enc_w1, out):
             )
 
         def square_scalar(r, i):
-            squares = rows.tile([P, D], F32)
+            squares = stage.tile([P, D], F32)
             nc.scalar.activation(
                 out=squares[:],
                 in_=h2_tiles[r][:, i, :],
@@ -370,6 +373,7 @@ def tile_mybadtransfomerblock_pa_t_kernel(tc, x, pos_emb, enc_w0, enc_w1, out):
                 square_scalar(r, i)
 
         for s in range(4, ROUNDS):
+            run(load_ahead, s + 4)
             transpose_x(s)
             scalar_stages(s - 4)
             if s - 2 < PAIRS:

@@ -64,13 +64,17 @@ def tile_mybadtransfomerblock_pa_t_kernel(tc, x, pos_emb, enc_w0, enc_w1, out):
             pair = slice(PAIR * q, PAIR * (q + 1))
             nc.sync.dma_start(out=pos_rows[:, pair, :], in_=pos_view[0, :, pair, :])
 
-        w0_view = enc_w0.rearrange("(u m e) k -> u m e k", u=HALVES, e=2)
-        for u in range(HALVES):
-            nc.sync.dma_start(out=w0_rows[:, 2 * u : 2 * u + 2, :], in_=w0_view[u])
+        def load_half(w_rows, w, u):
+            w_view = w.rearrange("(u m e) k -> u m e k", u=HALVES, e=2)
+            nc.sync.dma_start(out=w_rows[:, 2 * u : 2 * u + 2, :], in_=w_view[u])
+
+        load_half(w0_rows, enc_w0, 0)
         load_pos(0)
         load_x(0, 0, 1)
+        load_half(w0_rows, enc_w0, 1)
         load_x(1, 0, 1)
-        nc.sync.dma_start(out=w1_rows[:], in_=enc_w1.rearrange("(c m) k -> m c k", m=P))
+        for u in range(HALVES):
+            load_half(w1_rows, enc_w1, u)
         for q in range(1, PAIRS):
             load_x(q + 1, 0, 1)
             load_pos(q)
@@ -93,12 +97,13 @@ def tile_mybadtransfomerblock_pa_t_kernel(tc, x, pos_emb, enc_w0, enc_w1, out):
         warm = keep.tile([P, 1], F32)
         nc.scalar.activation(out=warm[:], in_=tiny[:], func=ACT.Sqrt)
 
-        def transpose_pair(src_rows, h, t_bank):
+        def transpose_pair(src_rows, h, t_bank, woven=False):
             src_words = src_rows[:].bitcast(F32)
             for i in range(PAIR):
+                columns = slice(i, ROUND_TOKENS, PAIR) if woven else slice(i * P, (i + 1) * P)
                 for u in range(HALVES):
                     nc.tensor.transpose(
-                        t_bank[:, i * P : (i + 1) * P, u],
+                        t_bank[:, columns, u],
                         src_words[:, PAIR * h + i, u * P : (u + 1) * P],
                         ident[:],
                     )
@@ -328,22 +333,26 @@ def tile_mybadtransfomerblock_pa_t_kernel(tc, x, pos_emb, enc_w0, enc_w1, out):
 
         idle_bank = psum_1.tile([P, D], F32, name="h1_bank")
         keep_awake(AWAKE_FIRST)
-        copy_grouped(nc.vector.tensor_copy, w0_grouped, 0, transpose_pair(w0_rows, 0, spare_bank_2()))
-        copy_grouped(nc.scalar.copy, w0_grouped, 1, transpose_pair(w0_rows, 1, spare_bank_2()))
-        prepare_pos(0, spare_bank_1())
-        transpose_x(0)
-        transpose_x(1)
-        keep_awake(2)
-        for h in range(2):
-            copy_grouped(nc.scalar.copy, w1_grouped, h, transpose_pair(w1_rows, h, spare_bank_2()))
-        for h in range(2):
+        def quantise_w0(h):
             half = slice(h * ROUND_TOKENS, (h + 1) * ROUND_TOKENS)
             quantise(w0_codes[:, half], w0_scales[:, half], w0_grouped[:, half, :])
+
+        copy_grouped(nc.vector.tensor_copy, w0_grouped, 0, transpose_pair(w0_rows, 0, spare_bank_2()))
+        prepare_pos(0, spare_bank_1())
+        transpose_x(0)
+        copy_grouped(nc.scalar.copy, w0_grouped, 1, transpose_pair(w0_rows, 1, spare_bank_2()))
+        transpose_x(1)
+        quantise_w0(0)
         add_pos(0)
-        add_pos(1)
         quantise_y(0)
-        quantise_y(1)
+        quantise_w0(1)
+        for h in range(2):
+            copy_grouped(
+                nc.scalar.copy, w1_grouped, h, transpose_pair(w1_rows, h, spare_bank_2(), woven=True)
+            )
         layer1(0)
+        add_pos(1)
+        quantise_y(1)
         open_h1(0)
         relu_h1_vector(0, 0)
         relu_h1_scalar(0, 1)
@@ -422,12 +431,12 @@ def tile_mybadtransfomerblock_pa_t_kernel(tc, x, pos_emb, enc_w0, enc_w1, out):
         invert_norm(LAST - 3)
         scale_and_store(LAST - 3)
         open_h2(LAST - 1)
-        relu_h2_vector(LAST - 1, 0)
+        relu_h2_scalar(LAST - 1, 0)
         relu_h2_vector(LAST - 1, 1)
         layer2(LAST)
         open_h2(LAST)
-        square_scalar(LAST - 1, 0)
         root_norm(LAST - 2)
+        square_scalar(LAST - 1, 0)
         relu_h2_vector(LAST, 0)
         pad_norm(LAST - 2)
         relu_h2_vector(LAST, 1)

from contextlib import ExitStack

import concourse.mybir as mybir
from concourse.masks import make_identity

BF16 = mybir.dt.bfloat16
F32 = mybir.dt.float32
U32 = mybir.dt.uint32
U8 = mybir.dt.uint8
FP8X4 = mybir.dt.float8_e4m3fn_x4
ACT = mybir.ActivationFunctionType
ALU = mybir.AluOpType

P = 128
PACK = 4
D = P * PACK
HALVES = 2
BATCH = 8
SEQ = 1024
TILES = SEQ // P
PAIR = 2
ROUND_TOKENS = PAIR * P
PAIRS = TILES // PAIR
ROUNDS = BATCH * PAIRS
LAST = ROUNDS - 1
AWAKE_FIRST = 6
EPS = 1e-6
TINY = 1e-30

FLOPS = 2 * 2 * BATCH * SEQ * D * D


def tile_mybadtransfomerblock_pa_t_kernel(tc, x, pos_emb, enc_w0, enc_w1, out):
    nc = tc.nc
    x_view = x.rearrange("b (p j) k -> b p j k", j=TILES)
    pos_view = pos_emb.rearrange("o (p j) k -> o p j k", j=TILES)
    out_view = out.rearrange("b (p j) f -> b p j f", j=TILES)

    def place(r):
        q, b = divmod(r, BATCH)
        return b, q

    with ExitStack() as ctx:
        keep = ctx.enter_context(tc.tile_pool(name="keep", bufs=1))
        stage = ctx.enter_context(tc.tile_pool(name="stage", bufs=2))
        rows = ctx.enter_context(tc.tile_pool(name="rows", bufs=12))
        psum_t = ctx.enter_context(tc.psum_pool(name="psum_t", bufs=2))
        psum_1 = ctx.enter_context(tc.psum_pool(name="psum_1", bufs=3))
        psum_2 = ctx.enter_context(tc.psum_pool(name="psum_2", bufs=3))
        ctx.enter_context(tc.manual_schedule())

        w0_rows = keep.tile([P, PACK, D], BF16)
        w1_rows = keep.tile([P, PACK, D], BF16)
        pos_rows = keep.tile([P, TILES, D], BF16)
        x_rows = [keep.tile([P, TILES, D], BF16, name="x%d" % b) for b in range(BATCH)]

        def load_x(b, first, last):
            nc.sync.dma_start(
                out=x_rows[b][:, PAIR * first : PAIR * last, :],
                in_=x_view[b, :, PAIR * first : PAIR * last, :],
            )

        def load_pos(q):
            pair = slice(PAIR * q, PAIR * (q + 1))
            nc.sync.dma_start(out=pos_rows[:, pair, :], in_=pos_view[0, :, pair, :])

        def load_half(w_rows, w, u):
            w_view = w.rearrange("(u m e) k -> u m e k", u=HALVES, e=2)
            nc.sync.dma_start(out=w_rows[:, 2 * u : 2 * u + 2, :], in_=w_view[u])

        load_half(w0_rows, enc_w0, 0)
        load_pos(0)
        load_x(0, 0, 1)
        load_half(w0_rows, enc_w0, 1)
        load_x(1, 0, 1)
        for u in range(HALVES):
            load_half(w1_rows, enc_w1, u)
        for q in range(1, PAIRS):
            load_x(q + 1, 0, 1)
            load_pos(q)
        for b in range(PAIRS + 1, BATCH):
            load_x(b, 0, 1)

        def load_ahead(r):
            b, q = place(r)
            if q == 1:
                load_x(b, 1, 2)
            elif q == 2:
                load_x(b, 2, PAIRS)

        zeros = keep.tile([P, D], BF16)
        nc.vector.memset(zeros[:], 0.0)
        ident = keep.tile([P, P], F32)
        make_identity(nc, ident[:])
        tiny = keep.tile([P, 1], F32)
        nc.vector.memset(tiny[:], TINY)
        warm = keep.tile([P, 1], F32)
        nc.scalar.activation(out=warm[:], in_=tiny[:], func=ACT.Sqrt)

        def transpose_pair(src_rows, h, t_bank, woven=False):
            src_words = src_rows[:].bitcast(F32)
            for i in range(PAIR):
                columns = slice(i, ROUND_TOKENS, PAIR) if woven else slice(i * P, (i + 1) * P)
                for u in range(HALVES):
                    nc.tensor.transpose(
                        t_bank[:, columns, u],
                        src_words[:, PAIR * h + i, u * P : (u + 1) * P],
                        ident[:],
                    )
            return t_bank

        def copy_grouped(copy, grouped, h, t_bank):
            copy(
                out=grouped[:].bitcast(F32)[:, h * ROUND_TOKENS : (h + 1) * ROUND_TOKENS, :],
                in_=t_bank[:],
            )

        def quantise(codes, scales, grouped):
            nc.vector.quantize_mx(
                out=codes.bitcast(FP8X4),
                scales=scales,
                in_=grouped.rearrange("p c t -> p (c t)"),
            )

        xt_banks, y_tiles, y_mx, h1_banks, h1_tiles, h1_mx = {}, {}, {}, {}, {}, {}
        h2_banks, h2_tiles, sumsqs, norms, paddeds, invs = {}, {}, {}, {}, {}, {}

        def transpose_x(r):
            b, q = place(r)
            t_bank = psum_t.tile([P, ROUND_TOKENS, HALVES], F32)
            xt_banks[r] = transpose_pair(x_rows[b], q, t_bank)

        def prepare_pos(q, t_bank):
            copy_grouped(nc.scalar.copy, pos_grouped, q, transpose_pair(pos_rows, q, t_bank))

        def add_pos(r):
            q = place(r)[1]
            y_grouped = stage.tile([P, ROUND_TOKENS, PACK], BF16, align_bytes=64)
            nc.vector.tensor_tensor(
                out=y_grouped[:],
                in0=xt_banks[r][:].bitcast(BF16),
                in1=pos_grouped[:, q * ROUND_TOKENS : (q + 1) * ROUND_TOKENS, :],
                op=ALU.add,
            )
            y_tiles[r] = y_grouped

        def quantise_y(r):
            y_codes = stage.tile([P, ROUND_TOKENS], U32, align_bytes=64)
            y_scales = stage.tile([P, ROUND_TOKENS], U8, align_bytes=64)
            quantise(y_codes[:], y_scales[:], y_tiles[r][:])
            y_mx[r] = y_codes, y_scales

        def layer1(r):
            y_codes, y_scales = y_mx[r]
            h1_banks[r] = []
            for i in range(PAIR):
                tokens = slice(i * P, (i + 1) * P)
                h1_bank = psum_1.tile([P, PACK, P], F32)
                for t in range(PACK):
                    nc.tensor.matmul_mx(
                        out=h1_bank[:, t, :],
                        lhsT=w0_codes[:, t * P : (t + 1) * P].bitcast(FP8X4),
                        lhsT_scale=w0_scales[:, t * P : (t + 1) * P],
                        rhs=y_codes[:, tokens].bitcast(FP8X4),
                        rhs_scale=y_scales[:, tokens],
                        start=True,
                        stop=True,
                    )
                h1_banks[r].append(h1_bank)

        def open_h1(r):
            h1_grouped = stage.tile([P, ROUND_TOKENS, PACK], BF16, align_bytes=64)
            h1_tiles[r] = h1_grouped

        def relu_h1_scalar(r, i):
            nc.scalar.activation(
                out=h1_tiles[r][:, i * P : (i + 1) * P, :],
                in_=h1_banks[r][i][:].rearrange("p t r -> p r t"),
                func=ACT.Relu,
            )

        def relu_h1_vector(r, i):
            nc.vector.tensor_scalar_max(
                out=h1_tiles[r][:, i * P : (i + 1) * P, :],
                in0=h1_banks[r][i][:].rearrange("p t r -> p r t"),
                scalar1=0.0,
            )

        def quantise_h1(r):
            h1_codes = stage.tile([P, ROUND_TOKENS], U32, align_bytes=64)
            h1_scales = stage.tile([P, ROUND_TOKENS], U8, align_bytes=64)
            quantise(h1_codes[:], h1_scales[:], h1_tiles[r][:])
            h1_mx[r] = h1_codes, h1_scales

        def layer2(r):
            h1_codes, h1_scales = h1_mx[r]
            h2_banks[r] = []
            for i in range(PAIR):
                tokens = slice(i * P, (i + 1) * P)
                if r < LAST:
                    h2_bank = psum_2.tile([P, D], F32)
                else:
                    t_bank = psum_t.tile([P, D], F32)
                    h2_bank = t_bank
                nc.tensor.matmul_mx(
                    out=h2_bank[:],
                    lhsT=h1_codes[:, tokens].bitcast(FP8X4),
                    lhsT_scale=h1_scales[:, tokens],
                    rhs=w1_codes[:].bitcast(FP8X4),
                    rhs_scale=w1_scales[:],
                    start=True,
                    stop=True,
                )
                h2_banks[r].append(h2_bank)

        def open_h2(r):
            h2_rows = rows.tile([P, PAIR, D], F32)
            sumsq = rows.tile([P, PAIR], F32)
            h2_tiles[r], sumsqs[r] = h2_rows, sumsq

        def relu_h2_scalar(r, i):
            nc.scalar.activation(out=h2_tiles[r][:, i, :], in_=h2_banks[r][i][:], func=ACT.Relu)

        def relu_h2_vector(r, i):
            nc.vector.tensor_scalar_max(
                out=h2_tiles[r][:, i, :], in0=h2_banks[r][i][:], scalar1=0.0
            )

        def square_scalar(r, i):
            squares = stage.tile([P, D], F32)
            nc.scalar.activation(
                out=squares[:],
                in_=h2_tiles[r][:, i, :],
                func=ACT.Square,
                accum_out=sumsqs[r][:, i : i + 1],
            )

        def square_vector(r, i):
            products = rows.tile([P, D], F32)
            nc.vector.scalar_tensor_tensor(
                out=products[:],
                in0=h2_tiles[r][:, i, :],
                scalar=1.0,
                in1=h2_tiles[r][:, i, :],
                op0=ALU.mult,
                op1=ALU.mult,
                accum_out=sumsqs[r][:, i : i + 1],
            )

        def root_norm(r):
            norm = rows.tile([P, PAIR], F32)
            nc.scalar.activation(out=norm[:], in_=sumsqs[r][:], func=ACT.Sqrt, bias=tiny[:])
            norms[r] = norm

        def pad_norm(r):
            padded = rows.tile([P, PAIR], F32)
            nc.vector.tensor_scalar_add(out=padded[:], in0=norms[r][:], scalar1=EPS)
            paddeds[r] = padded

        def pad_norm_scalar(r):
            padded = rows.tile([P, PAIR], F32)
            nc.scalar.activation(out=padded[:], in_=norms[r][:], func=ACT.Copy, bias=EPS)
            paddeds[r] = padded

        def invert_norm(r):
            inv = rows.tile([P, PAIR], F32)
            nc.vector.reciprocal(out=inv[:], in_=paddeds[r][:])
            invs[r] = inv

        def scale_vector(r, i):
            nc.vector.tensor_scalar_mul(
                out=h2_tiles[r][:, i, :], in0=h2_tiles[r][:, i, :], scalar1=invs[r][:, i : i + 1]
            )

        def scale_gpsimd(r, i):
            nc.gpsimd.tensor_scalar(
                out=h2_tiles[r][:, i, :],
                in0=h2_tiles[r][:, i, :],
                scalar1=invs[r][:, i : i + 1],
                scalar2=0.0,
                op0=ALU.mult,
                op1=ALU.add,
            )

        def scale_scalar(r, i):
            nc.scalar.activation(
                out=h2_tiles[r][:, i, :],
                in_=h2_tiles[r][:, i, :],
                func=ACT.Copy,
                scale=invs[r][:, i : i + 1],
            )

        def store(r):
            b, q = place(r)
            nc.sync.dma_start(
                out=out_view[b, :, PAIR * q : PAIR * (q + 1), :], in_=h2_tiles[r][:]
            )

        def store_tile(r, i):
            b, q = place(r)
            nc.sync.dma_start(out=out_view[b, :, PAIR * q + i, :], in_=h2_tiles[r][:, i, :])

        def scale_and_store(r):
            for i in range(PAIR):
                scale_gpsimd(r, i)
            store(r)

        def run(stage_fn, r, *rest):
            if 0 <= r < ROUNDS:
                stage_fn(r, *rest)

        w0_grouped = keep.tile([P, D, PACK], BF16, align_bytes=64)
        w1_grouped = keep.tile([P, D, PACK], BF16, align_bytes=64)
        w0_codes = keep.tile([P, D], U32, align_bytes=64)
        w0_scales = keep.tile([P, D], U8, align_bytes=64)
        w1_codes = keep.tile([P, D], U32, align_bytes=64)
        w1_scales = keep.tile([P, D], U8, align_bytes=64)
        pos_grouped = keep.tile([P, SEQ, PACK], BF16)

        def spare_bank_1():
            h1_bank = psum_1.tile([P, ROUND_TOKENS, HALVES], F32)
            return h1_bank

        def spare_bank_2():
            h2_bank = psum_2.tile([P, ROUND_TOKENS, HALVES], F32)
            return h2_bank

        def keep_awake(passes):
            for i in range(passes):
                nc.tensor.matmul(
                    idle_bank[:], lhsT=zeros[:, :P], rhs=zeros[:], start=True, stop=True
                )

        idle_bank = psum_1.tile([P, D], F32, name="h1_bank")
        keep_awake(AWAKE_FIRST)
        def quantise_w0(h):
            half = slice(h * ROUND_TOKENS, (h + 1) * ROUND_TOKENS)
            quantise(w0_codes[:, half], w0_scales[:, half], w0_grouped[:, half, :])

        copy_grouped(nc.vector.tensor_copy, w0_grouped, 0, transpose_pair(w0_rows, 0, spare_bank_2()))
        prepare_pos(0, spare_bank_1())
        transpose_x(0)
        copy_grouped(nc.scalar.copy, w0_grouped, 1, transpose_pair(w0_rows, 1, spare_bank_2()))
        transpose_x(1)
        quantise_w0(0)
        add_pos(0)
        quantise_y(0)
        quantise_w0(1)
        for h in range(2):
            copy_grouped(
                nc.scalar.copy, w1_grouped, h, transpose_pair(w1_rows, h, spare_bank_2(), woven=True)
            )
        layer1(0)
        add_pos(1)
        quantise_y(1)
        open_h1(0)
        relu_h1_vector(0, 0)
        relu_h1_scalar(0, 1)
        transpose_x(2)
        prepare_pos(1, spare_bank_2())
        layer1(1)
        quantise(w1_codes[:], w1_scales[:], w1_grouped[:])
        quantise_h1(0)
        layer2(0)
        transpose_x(3)
        add_pos(2)
        open_h1(1)
        relu_h1_vector(1, 0)
        relu_h1_scalar(1, 1)
        quantise_y(2)
        layer1(2)
        quantise_h1(1)

        def scalar_stages(r):
            open_h2(r)
            relu_h2_scalar(r, 0)
            run(root_norm, r - 1)
            relu_h2_scalar(r, 1)
            if r % 2 == 0:
                run(pad_norm_scalar, r - 1)
            for i in range(PAIR):
                square_scalar(r, i)

        for s in range(4, ROUNDS):
            run(load_ahead, s + 4)
            transpose_x(s)
            scalar_stages(s - 4)
            if s - 2 < PAIRS:
                prepare_pos(s - 2, spare_bank_2())
            add_pos(s - 1)
            if s % 2 == 0:
                run(pad_norm, s - 6)
            if s > 4:
                quantise_h1(s - 3)
            layer2(s - 3)
            quantise_y(s - 1)
            run(invert_norm, s - 6)
            open_h1(s - 2)
            for i in range(PAIR):
                relu_h1_vector(s - 2, i)
            layer1(s - 1)
            run(scale_and_store, s - 6)

        scalar_stages(LAST - 3)
        add_pos(LAST)
        pad_norm(LAST - 5)
        quantise_h1(LAST - 2)
        layer2(LAST - 2)
        quantise_y(LAST)
        invert_norm(LAST - 5)
        scale_and_store(LAST - 5)
        open_h1(LAST - 1)
        for i in range(PAIR):
            relu_h1_vector(LAST - 1, i)
        layer1(LAST)
        open_h2(LAST - 2)
        relu_h2_scalar(LAST - 2, 0)
        root_norm(LAST - 3)
        relu_h2_scalar(LAST - 2, 1)
        for i in range(PAIR):
            square_scalar(LAST - 2, i)
        quantise_h1(LAST - 1)
        layer2(LAST - 1)
        invert_norm(LAST - 4)
        scale_and_store(LAST - 4)
        open_h1(LAST)
        for i in range(PAIR):
            relu_h1_vector(LAST, i)
        pad_norm(LAST - 3)
        quantise_h1(LAST)
        invert_norm(LAST - 3)
        scale_and_store(LAST - 3)
        open_h2(LAST - 1)
        relu_h2_scalar(LAST - 1, 0)
        relu_h2_vector(LAST - 1, 1)
        layer2(LAST)
        open_h2(LAST)
        root_norm(LAST - 2)
        square_scalar(LAST - 1, 0)
        relu_h2_vector(LAST, 0)
        pad_norm(LAST - 2)
        relu_h2_vector(LAST, 1)
        invert_norm(LAST - 2)
        square_scalar(LAST - 1, 1)
        square_scalar(LAST, 0)
        root_norm(LAST - 1)
        square_scalar(LAST, 1)
        root_norm(LAST)
        for i in range(PAIR):
            scale_vector(LAST - 2, i)
        store(LAST - 2)
        pad_norm(LAST - 1)
        invert_norm(LAST - 1)
        scale_vector(LAST - 1, 0)
        pad_norm(LAST)
        scale_vector(LAST - 1, 1)
        store(LAST - 1)
        invert_norm(LAST)
        for i, scale in enumerate((scale_vector, scale_scalar)):
            scale(LAST, i)
            store_tile(LAST, i)
